import numpy as np
import ml_dtypes


def mxq(x, axis, fmt="e4m3"):
    dtype, down = {"e4m3": (ml_dtypes.float8_e4m3fn, 7), "e5m2": (ml_dtypes.float8_e5m2, 14)}[fmt]
    v = np.moveaxis(np.asarray(x, np.float32).astype(ml_dtypes.bfloat16).astype(np.float64), axis, -1)
    blocks = v.reshape(v.shape[:-1] + (-1, 32))
    amax = np.abs(blocks).max(-1, keepdims=True)
    byte = np.maximum(np.where(amax > 0, np.frexp(amax)[1] - 1 + 127, 0) - down, 1)
    scale = np.exp2(byte - 127.0)
    codes = (blocks / scale).astype(np.float32).astype(dtype).astype(np.float64)
    return np.moveaxis((codes * scale).reshape(v.shape), -1, axis)


WIDE = False


def mx_kscale(k):
    if not WIDE:
        return np.ones(k)
    levels = np.array([10, -10, 5, -5, 0])
    a = np.random.permutation(np.resize(levels, k // 512 * 4)).reshape(k // 512, 4)
    idx = np.arange(k)
    return np.exp2(a[idx // 512, idx % 128 // 32])


BF16 = ml_dtypes.bfloat16


def bf(x):
    return np.asarray(x, np.float32).astype(BF16)


def f64(x):
    return np.asarray(x).astype(np.float64)


B, R, N, D, L = 8, 2, 512, 512, 2
RN = R * N
P_EDGE = 0.02


def setup_inputs():
    s = mx_kscale(D)
    return {"x": bf(np.random.standard_normal((B, N, D)) * 0.6 * s),
            "adj": bf(np.random.random((B, R, N, N)) < P_EDGE),
            "wr": bf(np.random.standard_normal((R, D, D)) * 3.0 / np.sqrt(D) / s[:, None]),
            "br": bf(np.random.standard_normal((R, D)) * 0.3),
            "w0": bf(np.random.standard_normal((D, D)) * 3.0 / np.sqrt(D) / s[:, None]),
            "b0": bf(np.random.standard_normal(D) * 0.5)}


def reference(x, adj, wr, br, w0, b0):
    a = f64(adj)
    den = a.sum(axis=(1, 3))[:, :, None] + 1.0
    xq = mxq(f64(x), 2, "e4m3")
    msg = (xq[:, None] @ mxq(f64(wr), 1, "e4m3")[None]) + f64(br)[None, :, None, :]
    a_flat = a.transpose(0, 2, 1, 3).reshape(B, N, RN)
    agg = mxq(a_flat, 2, "e4m3") @ mxq(msg.reshape(B, RN, D), 1, "e4m3")
    self_term = (xq @ mxq(f64(w0), 0, "e4m3")) + f64(b0)
    return np.maximum((agg + self_term) / den, 0.0)

@@ -1,0 +1,204 @@
+from contextlib import ExitStack
+
+import concourse.mybir as mybir
+from concourse.masks import make_identity
+
+F32 = mybir.dt.float32
+BF16 = mybir.dt.bfloat16
+U32 = mybir.dt.uint32
+U8 = mybir.dt.uint8
+FP8X4 = mybir.dt.float8_e4m3fn_x4
+ADD = mybir.AluOpType.add
+ACT = mybir.ActivationFunctionType
+
+B, R, N, D = 8, 2, 512, 512
+P = 128
+S = 4
+FLOPS = 2 * B * (R * N * D * D + N * R * N * D + N * D * D)
+
+
+def tile_rgcn_layer_pa_t_kernel(tc, x, adj, wr, br, w0, b0, out):
+    nc = tc.nc
+    with ExitStack() as ctx:
+        const = ctx.enter_context(tc.tile_pool(name="const", bufs=1))
+        xin = ctx.enter_context(tc.tile_pool(name="xin", bufs=4))
+        ain = ctx.enter_context(tc.tile_pool(name="ain", bufs=4))
+        grp = ctx.enter_context(tc.tile_pool(name="grp", bufs=3))
+        qnt = ctx.enter_context(tc.tile_pool(name="qnt", bufs=2))
+        epi = ctx.enter_context(tc.tile_pool(name="epi", bufs=4))
+        res = ctx.enter_context(tc.tile_pool(name="res", bufs=3))
+        small = ctx.enter_context(tc.tile_pool(name="small", bufs=3))
+        ps_t = ctx.enter_context(tc.psum_pool(name="ps_t", bufs=3))
+        ps_m = ctx.enter_context(tc.psum_pool(name="ps_m", bufs=3))
+        ps_o = ctx.enter_context(tc.psum_pool(name="ps_o", bufs=2))
+
+        x_tiles = {}
+        a_tiles = {}
+
+        def load(b):
+            x_sb = xin.tile([P, S, D], BF16, name="x_sb")
+            nc.sync.dma_start(
+                out=x_sb[:].rearrange("p (u e) f -> p u (e f)", u=2),
+                in_=x[b].rearrange("(u p e) f -> p u (e f)", u=2, e=2),
+            )
+            a_sb = ain.tile([P, R, S, N], BF16, name="a_sb")
+            nc.sync.dma_start(
+                out=a_sb[:].rearrange("p r (u e) j -> p (r u) (e j)", u=2),
+                in_=adj[b].rearrange("r (u p e) j -> p (r u) (e j)", u=2, e=2),
+            )
+            x_tiles[b] = x_sb
+            a_tiles[b] = a_sb
+
+        ident = const.tile([P, P], F32, name="ident")
+        make_identity(nc, ident[:])
+        bias = const.tile([P, 3 * D], BF16, name="bias")
+        nc.scalar.dma_start(out=bias[:, 0 : 2 * D], in_=br.rearrange("r d -> (r d)").partition_broadcast(P))
+        nc.scalar.dma_start(out=bias[:, 2 * D : 3 * D], in_=b0.partition_broadcast(P))
+
+        x_sb0 = xin.tile([P, S, D], BF16, name="x_sb")
+        nc.sync.dma_start(
+            out=x_sb0[:].rearrange("p (u e) f -> p u (e f)", u=2),
+            in_=x[0].rearrange("(u p e) f -> p u (e f)", u=2, e=2),
+        )
+        x_tiles[0] = x_sb0
+        w_raw = const.tile([P, 3, S, D], BF16, name="w_raw")
+        for w in range(3):
+            src = wr[w] if w < R else w0
+            nc.sync.dma_start(
+                out=w_raw[:, w].rearrange("p (u e) c -> p u (e c)", u=2),
+                in_=src.rearrange("(u p e) c -> p u (e c)", u=2, e=2),
+            )
+        a_sb0 = ain.tile([P, R, S, N], BF16, name="a_sb")
+        nc.sync.dma_start(
+            out=a_sb0[:].rearrange("p r (u e) j -> p (r u) (e j)", u=2),
+            in_=adj[0].rearrange("r (u p e) j -> p (r u) (e j)", u=2, e=2),
+        )
+        a_tiles[0] = a_sb0
+        for b in range(1, 4):
+            load(b)
+
+        w_grp = const.tile([P, 3, D, S], BF16, name="w_grp", align_bytes=64)
+        w_words = const.tile([P, 3 * D], U32, name="w_words", align_bytes=64)
+        w_scales = const.tile([P, 3 * D], U8, name="w_scales", align_bytes=64)
+        for w in range(3):
+            nc.vector.tensor_copy(out=w_grp[:, w], in_=w_raw[:, w].rearrange("p t c -> p c t"))
+        for w in range(3):
+            nc.vector.quantize_mx(
+                out=w_words[:, w * D : (w + 1) * D].bitcast(FP8X4),
+                scales=w_scales[:, w * D : (w + 1) * D],
+                in_=w_grp[:, w].rearrange("p c t -> p (c t)"),
+            )
+
+        def transpose_unit(src_words, tag):
+            g = grp.tile([P, 512, 2], F32, name="g_" + tag, tag="g_" + tag, align_bytes=64)
+            for h in range(2):
+                bank = ps_t.tile([P, 2, 256], F32, name="bank_t")
+                for sl in range(2):
+                    for u in range(2):
+                        nc.tensor.transpose(
+                            bank[:, u, sl * P : (sl + 1) * P],
+                            src_words[:, 2 * h + sl, u * P : (u + 1) * P],
+                            ident[:],
+                        )
+                nc.scalar.copy(out=g[:, h * 256 : (h + 1) * 256, :], in_=bank[:].rearrange("p u c -> p c u"))
+            return g
+
+        def quantise(g_bf16, tag):
+            words = qnt.tile([P, 512], U32, name="w_" + tag, tag="w_" + tag, align_bytes=64)
+            scales = qnt.tile([P, 512], U8, name="s_" + tag, tag="s_" + tag, align_bytes=64)
+            nc.vector.quantize_mx(out=words[:].bitcast(FP8X4), scales=scales[:], in_=g_bf16)
+            return words, scales
+
+        xq = {}
+        aq = {}
+        mq = {}
+        rdens = {}
+
+        def stage_a(b):
+            xw = x_tiles[b][:].bitcast(F32)
+            aw = a_tiles[b][:].bitcast(F32)
+            gx = transpose_unit(xw, "x")
+            ga = [transpose_unit(aw[:, r], "a") for r in range(R)]
+            xq[b] = quantise(gx[:].rearrange("p c u -> p (c u)").bitcast(BF16), "x")
+            for r in range(R):
+                aq[(b, r)] = quantise(ga[r][:].rearrange("p c u -> p (c u)").bitcast(BF16), "a%d" % r)
+            dsum = small.tile([P, S], F32, name="dsum")
+            for s in range(S):
+                junk = small.tile([P, R, N], BF16, name="junk")
+                nc.scalar.activation(
+                    out=junk[:], in_=a_tiles[b][:, :, s, :], func=ACT.Copy, accum_out=dsum[:, s : s + 1]
+                )
+            den = small.tile([P, S], F32, name="den")
+            nc.vector.tensor_scalar_add(den[:], dsum[:], 1.0)
+            rden = small.tile([P, S], F32, name="rden")
+            nc.vector.reciprocal(rden[:], den[:])
+            rdens[b] = rden
+
+        def stage_msg(b):
+            xw, xs = xq[b]
+            for r in range(R):
+                mg = grp.tile([P, D, S], BF16, name="mg", align_bytes=64)
+                for dc in range(4):
+                    bank = ps_m.tile([P, S, P], F32, name="bank_m")
+                    cols = slice(r * D + dc * P, r * D + (dc + 1) * P)
+                    for s in range(S):
+                        nc.tensor.matmul_mx(
+                            out=bank[:, s, :],
+                            lhsT=xw[:, s * P : (s + 1) * P].bitcast(FP8X4),
+                            lhsT_scale=xs[:, s * P : (s + 1) * P],
+                            rhs=w_words[:, cols].bitcast(FP8X4),
+                            rhs_scale=w_scales[:, cols],
+                            start=True,
+                            stop=True,
+                        )
+                    nc.vector.tensor_tensor(
+                        out=mg[:, dc * P : (dc + 1) * P, :],
+                        in0=bank[:].rearrange("p s d -> p d s"),
+                        in1=bias[:, cols].unsqueeze(2).to_broadcast([P, P, S]),
+                        op=ADD,
+                    )
+                mq[(b, r)] = quantise(mg[:].rearrange("p d s -> p (d s)"), "m%d" % r)
+
+        def stage_agg(b):
+            xw, xs = xq[b]
+            o_sb = res.tile([P, S, D], F32, name="o_sb")
+            for s in range(S):
+                rows = slice(s * P, (s + 1) * P)
+                bank = ps_o.tile([P, D], F32, name="bank_o")
+                nc.tensor.matmul_mx(
+                    out=bank[:],
+                    lhsT=xw[:, rows].bitcast(FP8X4),
+                    lhsT_scale=xs[:, rows],
+                    rhs=w_words[:, 2 * D : 3 * D].bitcast(FP8X4),
+                    rhs_scale=w_scales[:, 2 * D : 3 * D],
+                    start=True,
+                    stop=False,
+                )
+                for r in range(R):
+                    aw, asc = aq[(b, r)]
+                    mw, msc = mq[(b, r)]
+                    nc.tensor.matmul_mx(
+                        out=bank[:],
+                        lhsT=aw[:, rows].bitcast(FP8X4),
+                        lhsT_scale=asc[:, rows],
+                        rhs=mw[:].bitcast(FP8X4),
+                        rhs_scale=msc[:],
+                        start=False,
+                        stop=(r == R - 1),
+                    )
+                t = epi.tile([P, D], F32, name="t")
+                nc.vector.tensor_tensor(out=t[:], in0=bank[:], in1=bias[:, 2 * D : 3 * D], op=ADD)
+                nc.scalar.activation(out=o_sb[:, s, :], in_=t[:], func=ACT.Relu, scale=rdens[b][:, s : s + 1])
+            nc.scalar.dma_start(
+                out=out[b].rearrange("(u p e) d -> p u (e d)", u=2, e=2),
+                in_=o_sb[:].rearrange("p (u e) d -> p u (e d)", u=2),
+            )
+
+        stage_a(0)
+        for b in range(B):
+            stage_msg(b)
+            if b + 1 < B:
+                stage_a(b + 1)
+            if b + 4 < B:
+                load(b + 4)
+            stage_agg(b)

@@ -8,197 +8,372 @@ BF16 = mybir.dt.bfloat16
 U32 = mybir.dt.uint32
 U8 = mybir.dt.uint8
 FP8X4 = mybir.dt.float8_e4m3fn_x4
-ADD = mybir.AluOpType.add
+ALU = mybir.AluOpType
 ACT = mybir.ActivationFunctionType
 
-B, R, N, D = 8, 2, 512, 512
-P = 128
-S = 4
+B, R, S = 8, 2, 4
+N, D, P = 512, 512, 128
 FLOPS = 2 * B * (R * N * D * D + N * R * N * D + N * D * D)
+CFG = {}
+
+
+def program(cfg):
+    ops = []
+    add = ops.append
+    fpaths = cfg.get("fpath", ["VSVS", "VSVS"])
+    wg1 = cfg.get("wg1", "SS")
+    wg2 = cfg.get("wg2", "GGGG")
+    h0 = cfg.get("h0", "SSSS")
+
+    def t(unit, k):
+        if 0 <= k < B:
+            add(("T", unit, k, 0))
+            add(("T", unit, k, 1))
+
+    def c(unit, k):
+        if 0 <= k < B:
+            add(("C", unit, k, 0))
+            add(("C", unit, k, 1))
+
+    def q(unit, k):
+        if 0 <= k < B:
+            add(("Q", unit, k))
+
+    def m(b, r, dc):
+        if b < B:
+            add(("M", b, r, dc))
+
+    def h(k, s):
+        if 1 <= k < B:
+            add(("H", k, s, "S"))
+
+    def ld(kind, k):
+        if k < B:
+            add((kind, k))
+
+    def f(b, s):
+        add(("F", b, s, fpaths[b % 2][s]))
+
+    def finish(b):
+        ld("LDA", b + 3); ld("LDX", b + 4)
+        add(("B", b, 0))
+        add(("SELF", b, 3)); add(("G", b, 3))
+        m(b + 1, 0, 1); m(b + 1, 0, 2)
+        t(2, b + 1)
+        add(("B", b, 1))
+        f(b, 0)
+        f(b, 1)
+        add(("ST", b, 0))
+        q(1, b + 1)
+        h(b + 1, 3)
+        add(("B", b, 2))
+        add(("B", b, 3))
+        f(b, 2)
+        f(b, 3)
+        add(("ST", b, 1))
+
+    add(("BIAS0",))
+    add(("LDX", 0)); add(("LDW", 0)); add(("LDW", 1)); add(("LDX", 1)); add(("LDA", 0)); add(("LDW", 2))
+    add(("LDA", 1)); add(("LDX", 2)); add(("LDA", 2)); add(("LDX", 3))
+    add(("BIAS",))
+    t(0, 0)
+    add(("C", 0, 0, 0)); add(("C", 0, 0, 1, "V"))
+    add(("WG", 0, "V", 0, 2)); add(("WG", 0, "S", 2, 4))
+    q(0, 0)
+    add(("WQ", 0, 0, 2))
+    m(0, 0, 0); m(0, 0, 1)
+    add(("WQ", 0, 2, 4))
+    m(0, 0, 2)
+    add(("WG", 1, wg1[0], 0, 2)); add(("WG", 1, wg1[1], 2, 4))
+    t(0, 1)
+    c(0, 1)
+    add(("A", 0, 0, 0)); m(0, 0, 3)
+    add(("A", 0, 0, 1))
+    add(("A", 0, 0, 2))
+    add(("A", 0, 0, 3))
+    t(1, 0); c(1, 0)
+    q(0, 1)
+    add(("WQ", 1, 0, 4))
+    m(0, 1, 0); m(0, 1, 1); m(0, 1, 2)
+    add(("QM", 0, 0))
+    for i in range(4):
+        add(("WG", 2, wg2[i], i, i + 1))
+    t(2, 0); c(2, 0)
+    add(("A", 0, 1, 0)); m(0, 1, 3)
+    add(("H", 0, 0, h0[0]))
+    add(("A", 0, 1, 1)); m(1, 0, 0)
+    add(("H", 0, 1, h0[1]))
+    add(("A", 0, 1, 2))
+    add(("A", 0, 1, 3))
+    t(0, 2); c(0, 2)
+    q(1, 0)
+    add(("WQ", 2, 0, 4))
+    for s in range(3):
+        add(("SELF", 0, s))
+    add(("QM", 0, 1))
+    q(2, 0)
+    add(("H", 0, 2, h0[2]))
+    add(("H", 0, 3, h0[3]))
+    for s in range(3):
+        add(("G", 0, s))
+    t(1, 1); c(1, 1)
+    q(0, 2)
+    add(("RD", 0))
+    h(1, 0); h(1, 1); h(1, 2)
+    finish(0)
+    for b in range(1, B):
+        add(("A", b, 0, 0)); m(b, 0, 3)
+        c(2, b)
+        add(("A", b, 0, 1)); m(b, 1, 0)
+        add(("A", b, 0, 2)); m(b, 1, 1)
+        add(("A", b, 0, 3)); m(b, 1, 2)
+        h(b + 1, 0)
+        add(("A", b, 1, 0)); m(b, 1, 3)
+        add(("QM", b, 0))
+        t(0, b + 2)
+        c(0, b + 2)
+        add(("A", b, 1, 1)); m(b + 1, 0, 0)
+        for s in range(3):
+            add(("SELF", b, s))
+        h(b + 1, 1)
+        add(("A", b, 1, 2))
+        t(1, b + 1)
+        add(("A", b, 1, 3))
+        q(2, b)
+        add(("QM", b, 1))
+        c(1, b + 1)
+        for s in range(3):
+            add(("G", b, s))
+        q(0, b + 2)
+        add(("RD", b))
+        h(b + 1, 2)
+        finish(b)
+    return ops
 
 
 def tile_rgcn_layer_pa_t_kernel(tc, x, adj, wr, br, w0, b0, out):
     nc = tc.nc
     with ExitStack() as ctx:
-        const = ctx.enter_context(tc.tile_pool(name="const", bufs=1))
-        xin = ctx.enter_context(tc.tile_pool(name="xin", bufs=4))
-        ain = ctx.enter_context(tc.tile_pool(name="ain", bufs=4))
-        grp = ctx.enter_context(tc.tile_pool(name="grp", bufs=3))
-        qnt = ctx.enter_context(tc.tile_pool(name="qnt", bufs=2))
-        epi = ctx.enter_context(tc.tile_pool(name="epi", bufs=4))
-        res = ctx.enter_context(tc.tile_pool(name="res", bufs=3))
-        small = ctx.enter_context(tc.tile_pool(name="small", bufs=3))
-        ps_t = ctx.enter_context(tc.psum_pool(name="ps_t", bufs=3))
+        pool = {}
+        for name, bufs in (("const", 1), ("b2", 2), ("b3", 3), ("b4", 4), ("b6", 6)):
+            pool[name] = ctx.enter_context(tc.tile_pool(name=name, bufs=bufs))
+        ps_t = ctx.enter_context(tc.psum_pool(name="ps_t", bufs=2))
         ps_m = ctx.enter_context(tc.psum_pool(name="ps_m", bufs=3))
-        ps_o = ctx.enter_context(tc.psum_pool(name="ps_o", bufs=2))
-
-        x_tiles = {}
-        a_tiles = {}
-
-        def load(b):
-            x_sb = xin.tile([P, S, D], BF16, name="x_sb")
-            nc.sync.dma_start(
-                out=x_sb[:].rearrange("p (u e) f -> p u (e f)", u=2),
-                in_=x[b].rearrange("(u p e) f -> p u (e f)", u=2, e=2),
-            )
-            a_sb = ain.tile([P, R, S, N], BF16, name="a_sb")
-            nc.sync.dma_start(
-                out=a_sb[:].rearrange("p r (u e) j -> p (r u) (e j)", u=2),
-                in_=adj[b].rearrange("r (u p e) j -> p (r u) (e j)", u=2, e=2),
-            )
-            x_tiles[b] = x_sb
-            a_tiles[b] = a_sb
-
+        ps_o = ctx.enter_context(tc.psum_pool(name="ps_o", bufs=3))
+        const = pool["const"]
         ident = const.tile([P, P], F32, name="ident")
         make_identity(nc, ident[:])
+        ctx.enter_context(tc.manual_schedule())
+        ones = const.tile([P, P], BF16, name="ones")
+        zb = const.tile([P, 3 * D], BF16, name="zb")
         bias = const.tile([P, 3 * D], BF16, name="bias")
-        nc.scalar.dma_start(out=bias[:, 0 : 2 * D], in_=br.rearrange("r d -> (r d)").partition_broadcast(P))
-        nc.scalar.dma_start(out=bias[:, 2 * D : 3 * D], in_=b0.partition_broadcast(P))
-
-        x_sb0 = xin.tile([P, S, D], BF16, name="x_sb")
-        nc.sync.dma_start(
-            out=x_sb0[:].rearrange("p (u e) f -> p u (e f)", u=2),
-            in_=x[0].rearrange("(u p e) f -> p u (e f)", u=2, e=2),
-        )
-        x_tiles[0] = x_sb0
         w_raw = const.tile([P, 3, S, D], BF16, name="w_raw")
-        for w in range(3):
+        w_grp = const.tile([P, 3, D, S], BF16, name="w_grp", align_bytes=64)
+        w_words = const.tile([P, 3 * D], U32, name="w_words", align_bytes=64)
+        w_scales = const.tile([P, 3 * D], U8, name="w_scales", align_bytes=64)
+
+        tl = {}
+
+        def copy_on(e, out_ap, in_ap):
+            if e == "S":
+                nc.scalar.copy(out=out_ap, in_=in_ap)
+            else:
+                nc.vector.tensor_copy(out=out_ap, in_=in_ap)
+
+        def op_ldx(k):
+            x_sb = pool["b4"].tile([P, S, D], BF16, name="x_sb")
+            nc.sync.dma_start(
+                out=x_sb[:].rearrange("p (u e) f -> p u (e f)", u=2),
+                in_=x[k].rearrange("(u p e) f -> p u (e f)", u=2, e=2),
+            )
+            tl[("x", k)] = x_sb
+
+        def op_lda(k):
+            a_sb = pool["b4"].tile([P, R, S, N], BF16, name="a_sb")
+            nc.sync.dma_start(
+                out=a_sb[:].rearrange("p r (u e) j -> p (r u) (e j)", u=2),
+                in_=adj[k].rearrange("r (u p e) j -> p (r u) (e j)", u=2, e=2),
+            )
+            tl[("a", k)] = a_sb
+
+        def op_ldw(w):
             src = wr[w] if w < R else w0
             nc.sync.dma_start(
                 out=w_raw[:, w].rearrange("p (u e) c -> p u (e c)", u=2),
                 in_=src.rearrange("(u p e) c -> p u (e c)", u=2, e=2),
             )
-        a_sb0 = ain.tile([P, R, S, N], BF16, name="a_sb")
-        nc.sync.dma_start(
-            out=a_sb0[:].rearrange("p r (u e) j -> p (r u) (e j)", u=2),
-            in_=adj[0].rearrange("r (u p e) j -> p (r u) (e j)", u=2, e=2),
-        )
-        a_tiles[0] = a_sb0
-        for b in range(1, 4):
-            load(b)
 
-        w_grp = const.tile([P, 3, D, S], BF16, name="w_grp", align_bytes=64)
-        w_words = const.tile([P, 3 * D], U32, name="w_words", align_bytes=64)
-        w_scales = const.tile([P, 3 * D], U8, name="w_scales", align_bytes=64)
-        for w in range(3):
-            nc.vector.tensor_copy(out=w_grp[:, w], in_=w_raw[:, w].rearrange("p t c -> p c t"))
-        for w in range(3):
+        def op_bias0():
+            nc.vector.memset(zb[:], 0.0)
+            nc.vector.memset(ones[:], 1.0)
+            nc.scalar.dma_start(out=zb[0:1, 0 : 2 * D], in_=br.rearrange("r d -> (r d)").unsqueeze(0))
+            nc.scalar.dma_start(out=zb[0:1, 2 * D : 3 * D], in_=b0.unsqueeze(0))
+
+        def op_bias():
+            for w in range(3):
+                bank = ps_o.tile([P, D], F32, name="bank_o")
+                nc.tensor.matmul(out=bank[:], lhsT=ones[:], rhs=zb[:, w * D : (w + 1) * D], start=True, stop=True)
+                copy_on("SVS"[w], bias[:, w * D : (w + 1) * D], bank[:])
+
+        def op_wg(w, e, c0, c1):
+            cols = slice(c0 * P, c1 * P)
+            if e == "G":
+                nc.gpsimd.tensor_scalar(
+                    out=w_grp[:, w, cols, :],
+                    in0=w_raw[:, w, :, cols].rearrange("p t c -> p c t"),
+                    scalar1=1.0,
+                    scalar2=0.0,
+                    op0=ALU.mult,
+                    op1=ALU.add,
+                )
+            else:
+                copy_on(
+                    e,
+                    w_grp[:, w, cols, :].rearrange("p (c i) t -> p c t i", i=4),
+                    w_raw[:, w, :, cols].rearrange("p t (c i) -> p c t i", i=4),
+                )
+
+        def op_wq(w, c0, c1):
+            cols = slice(w * D + c0 * P, w * D + c1 * P)
             nc.vector.quantize_mx(
-                out=w_words[:, w * D : (w + 1) * D].bitcast(FP8X4),
-                scales=w_scales[:, w * D : (w + 1) * D],
-                in_=w_grp[:, w].rearrange("p c t -> p (c t)"),
+                out=w_words[:, cols].bitcast(FP8X4),
+                scales=w_scales[:, cols],
+                in_=w_grp[:, w, c0 * P : c1 * P, :].rearrange("p c t -> p (c t)"),
             )
 
-        def transpose_unit(src_words, tag):
-            g = grp.tile([P, 512, 2], F32, name="g_" + tag, tag="g_" + tag, align_bytes=64)
-            for h in range(2):
-                bank = ps_t.tile([P, 2, 256], F32, name="bank_t")
-                for sl in range(2):
-                    for u in range(2):
-                        nc.tensor.transpose(
-                            bank[:, u, sl * P : (sl + 1) * P],
-                            src_words[:, 2 * h + sl, u * P : (u + 1) * P],
-                            ident[:],
-                        )
-                nc.scalar.copy(out=g[:, h * 256 : (h + 1) * 256, :], in_=bank[:].rearrange("p u c -> p c u"))
-            return g
+        def op_t(u, k, h):
+            if u == 0:
+                src = tl[("x", k)][:].bitcast(F32)
+            else:
+                src = tl[("a", k)][:].bitcast(F32)[:, u - 1]
+            bank = ps_t.tile([P, 2, 256], F32, name="bank_t")
+            for sl in range(2):
+                for w in range(2):
+                    nc.tensor.transpose(
+                        bank[:, w, sl * P : (sl + 1) * P], src[:, 2 * h + sl, w * P : (w + 1) * P], ident[:]
+                    )
+            tl[("bt", u, k, h)] = bank
 
-        def quantise(g_bf16, tag):
-            words = qnt.tile([P, 512], U32, name="w_" + tag, tag="w_" + tag, align_bytes=64)
-            scales = qnt.tile([P, 512], U8, name="s_" + tag, tag="s_" + tag, align_bytes=64)
+        def op_c(u, k, h, e="S"):
+            if h == 0:
+                tl[("g", u, k)] = pool["b2"].tile([P, 512, 2], F32, name="g%d" % u, align_bytes=64)
+            g = tl[("g", u, k)]
+            copy_on(e, g[:, h * 256 : (h + 1) * 256, :], tl[("bt", u, k, h)][:].rearrange("p w c -> p c w"))
+
+        def quantise(g_bf16, tag, bufs):
+            words = pool[bufs].tile([P, 512], U32, name="w_" + tag, align_bytes=64)
+            scales = pool[bufs].tile([P, 512], U8, name="s_" + tag, align_bytes=64)
             nc.vector.quantize_mx(out=words[:].bitcast(FP8X4), scales=scales[:], in_=g_bf16)
             return words, scales
 
-        xq = {}
-        aq = {}
-        mq = {}
-        rdens = {}
-
-        def stage_a(b):
-            xw = x_tiles[b][:].bitcast(F32)
-            aw = a_tiles[b][:].bitcast(F32)
-            gx = transpose_unit(xw, "x")
-            ga = [transpose_unit(aw[:, r], "a") for r in range(R)]
-            xq[b] = quantise(gx[:].rearrange("p c u -> p (c u)").bitcast(BF16), "x")
-            for r in range(R):
-                aq[(b, r)] = quantise(ga[r][:].rearrange("p c u -> p (c u)").bitcast(BF16), "a%d" % r)
-            dsum = small.tile([P, S], F32, name="dsum")
-            for s in range(S):
-                junk = small.tile([P, R, N], BF16, name="junk")
-                nc.scalar.activation(
-                    out=junk[:], in_=a_tiles[b][:, :, s, :], func=ACT.Copy, accum_out=dsum[:, s : s + 1]
-                )
-            den = small.tile([P, S], F32, name="den")
-            nc.vector.tensor_scalar_add(den[:], dsum[:], 1.0)
-            rden = small.tile([P, S], F32, name="rden")
-            nc.vector.reciprocal(rden[:], den[:])
-            rdens[b] = rden
-
-        def stage_msg(b):
-            xw, xs = xq[b]
-            for r in range(R):
-                mg = grp.tile([P, D, S], BF16, name="mg", align_bytes=64)
-                for dc in range(4):
-                    bank = ps_m.tile([P, S, P], F32, name="bank_m")
-                    cols = slice(r * D + dc * P, r * D + (dc + 1) * P)
-                    for s in range(S):
-                        nc.tensor.matmul_mx(
-                            out=bank[:, s, :],
-                            lhsT=xw[:, s * P : (s + 1) * P].bitcast(FP8X4),
-                            lhsT_scale=xs[:, s * P : (s + 1) * P],
-                            rhs=w_words[:, cols].bitcast(FP8X4),
-                            rhs_scale=w_scales[:, cols],
-                            start=True,
-                            stop=True,
-                        )
-                    nc.vector.tensor_tensor(
-                        out=mg[:, dc * P : (dc + 1) * P, :],
-                        in0=bank[:].rearrange("p s d -> p d s"),
-                        in1=bias[:, cols].unsqueeze(2).to_broadcast([P, P, S]),
-                        op=ADD,
-                    )
-                mq[(b, r)] = quantise(mg[:].rearrange("p d s -> p (d s)"), "m%d" % r)
-
-        def stage_agg(b):
-            xw, xs = xq[b]
-            o_sb = res.tile([P, S, D], F32, name="o_sb")
-            for s in range(S):
-                rows = slice(s * P, (s + 1) * P)
-                bank = ps_o.tile([P, D], F32, name="bank_o")
-                nc.tensor.matmul_mx(
-                    out=bank[:],
-                    lhsT=xw[:, rows].bitcast(FP8X4),
-                    lhsT_scale=xs[:, rows],
-                    rhs=w_words[:, 2 * D : 3 * D].bitcast(FP8X4),
-                    rhs_scale=w_scales[:, 2 * D : 3 * D],
-                    start=True,
-                    stop=False,
-                )
-                for r in range(R):
-                    aw, asc = aq[(b, r)]
-                    mw, msc = mq[(b, r)]
-                    nc.tensor.matmul_mx(
-                        out=bank[:],
-                        lhsT=aw[:, rows].bitcast(FP8X4),
-                        lhsT_scale=asc[:, rows],
-                        rhs=mw[:].bitcast(FP8X4),
-                        rhs_scale=msc[:],
-                        start=False,
-                        stop=(r == R - 1),
-                    )
-                t = epi.tile([P, D], F32, name="t")
-                nc.vector.tensor_tensor(out=t[:], in0=bank[:], in1=bias[:, 2 * D : 3 * D], op=ADD)
-                nc.scalar.activation(out=o_sb[:, s, :], in_=t[:], func=ACT.Relu, scale=rdens[b][:, s : s + 1])
-            nc.scalar.dma_start(
-                out=out[b].rearrange("(u p e) d -> p u (e d)", u=2, e=2),
-                in_=o_sb[:].rearrange("p (u e) d -> p u (e d)", u=2),
+        def op_q(u, k):
+            g = tl[("g", u, k)]
+            tl[("q", u, k)] = quantise(
+                g[:].rearrange("p c w -> p (c w)").bitcast(BF16), "q%d" % u, "b3" if u == 0 else "b2"
             )
 
-        stage_a(0)
-        for b in range(B):
-            stage_msg(b)
-            if b + 1 < B:
-                stage_a(b + 1)
-            if b + 4 < B:
-                load(b + 4)
-            stage_agg(b)
+        def op_h(k, s, e):
+            if ("dsum", k) not in tl:
+                tl[("dsum", k)] = pool["b3"].tile([P, S], F32, name="dsum")
+            junk = pool["b2"].tile([P, R, N], BF16, name="junk")
+            nc.scalar.activation(
+                out=junk[:], in_=tl[("a", k)][:, :, s, :], func=ACT.Copy, accum_out=tl[("dsum", k)][:, s : s + 1]
+            )
+
+        def op_rd(k):
+            den = pool["b3"].tile([P, S], F32, name="den")
+            nc.vector.tensor_scalar_add(den[:], tl[("dsum", k)][:], 1.0)
+            rden = pool["b3"].tile([P, S], F32, name="rden")
+            nc.vector.reciprocal(rden[:], den[:])
+            tl[("rden", k)] = rden
+
+        def op_m(b, r, dc):
+            xw, xs = tl[("q", 0, b)]
+            bank = ps_m.tile([P, S, P], F32, name="bank_m")
+            cols = slice(r * D + dc * P, r * D + (dc + 1) * P)
+            for s in range(S):
+                nc.tensor.matmul_mx(
+                    out=bank[:, s, :],
+                    lhsT=xw[:, s * P : (s + 1) * P].bitcast(FP8X4),
+                    lhsT_scale=xs[:, s * P : (s + 1) * P],
+                    rhs=w_words[:, cols].bitcast(FP8X4),
+                    rhs_scale=w_scales[:, cols],
+                    start=True,
+                    stop=True,
+                )
+            tl[("bm", b, r, dc)] = bank
+
+        def op_a(b, r, dc):
+            if dc == 0:
+                tl[("mg", b, r)] = pool["b2"].tile([P, D, S], BF16, name="mg", align_bytes=64)
+            cols = slice(r * D + dc * P, r * D + (dc + 1) * P)
+            nc.vector.tensor_tensor(
+                out=tl[("mg", b, r)][:, dc * P : (dc + 1) * P, :],
+                in0=tl[("bm", b, r, dc)][:].rearrange("p s d -> p d s"),
+                in1=bias[:, cols].unsqueeze(2).to_broadcast([P, P, S]),
+                op=ALU.add,
+            )
+
+        def op_qm(b, r):
+            tl[("qm", b, r)] = quantise(tl[("mg", b, r)][:].rearrange("p d s -> p (d s)"), "qm%d" % r, "b2")
+
+        def op_self(b, s):
+            xw, xs = tl[("q", 0, b)]
+            rows = slice(s * P, (s + 1) * P)
+            bank = ps_o.tile([P, D], F32, name="bank_o")
+            nc.tensor.matmul_mx(
+                out=bank[:],
+                lhsT=xw[:, rows].bitcast(FP8X4),
+                lhsT_scale=xs[:, rows],
+                rhs=w_words[:, 2 * D : 3 * D].bitcast(FP8X4),
+                rhs_scale=w_scales[:, 2 * D : 3 * D],
+                start=True,
+                stop=False,
+            )
+            tl[("bo", b, s)] = bank
+
+        def op_g(b, s):
+            rows = slice(s * P, (s + 1) * P)
+            for r in range(R):
+                aw, asc = tl[("q", 1 + r, b)]
+                mw, msc = tl[("qm", b, r)]
+                nc.tensor.matmul_mx(
+                    out=tl[("bo", b, s)][:],
+                    lhsT=aw[:, rows].bitcast(FP8X4),
+                    lhsT_scale=asc[:, rows],
+                    rhs=mw[:].bitcast(FP8X4),
+                    rhs_scale=msc[:],
+                    start=False,
+                    stop=(r == R - 1),
+                )
+
+        def op_b(b, s):
+            t = pool["b4"].tile([P, D], F32, name="t")
+            nc.vector.tensor_tensor(out=t[:], in0=tl[("bo", b, s)][:], in1=bias[:, 2 * D : 3 * D], op=ALU.add)
+            tl[("t", b, s)] = t
+
+        def op_f(b, s, e):
+            if ("o", b, s // 2) not in tl:
+                tl[("o", b, s // 2)] = pool["b6"].tile([P, 2, D], F32, name="o_sb")
+            o_ap = tl[("o", b, s // 2)][:, s % 2, :]
+            rd = tl[("rden", b)][:, s : s + 1]
+            if e == "S":
+                nc.scalar.activation(out=o_ap, in_=tl[("t", b, s)][:], func=ACT.Relu, scale=rd)
+            else:
+                nc.vector.tensor_scalar(
+                    out=o_ap, in0=tl[("t", b, s)][:], scalar1=rd, scalar2=0.0, op0=ALU.mult, op1=ALU.max
+                )
+
+        def op_st(b, u):
+            nc.scalar.dma_start(
+                out=out[b, 256 * u : 256 * (u + 1), :].rearrange("(p e) d -> p (e d)", e=2),
+                in_=tl[("o", b, u)][:].rearrange("p e d -> p (e d)"),
+            )
+
+        table = {
+            "LDX": op_ldx, "LDA": op_lda, "LDW": op_ldw, "BIAS0": op_bias0, "BIAS": op_bias, "WG": op_wg, "WQ": op_wq, "T": op_t,
+            "C": op_c, "Q": op_q, "H": op_h, "RD": op_rd, "M": op_m, "A": op_a, "QM": op_qm, "SELF": op_self,
+            "G": op_g, "B": op_b, "F": op_f, "ST": op_st,
+        }
+        for op in program(CFG):
+            table[op[0]](*op[1:])

@@ -14,14 +14,22 @@ ACT = mybir.ActivationFunctionType
 B, R, S = 8, 2, 4
 N, D, P = 512, 512, 128
 FLOPS = 2 * B * (R * N * D * D + N * R * N * D + N * D * D)
+FLT_MAX = 3.4028234663852886e38
 CFG = {}
 
 
 def program(cfg):
     ops = []
     add = ops.append
-    fpaths = cfg.get("fpath", ["VSVS", "VSVS"])
-    wg1 = cfg.get("wg1", "SS")
+    fpaths = cfg.get("fpath", ["SGGG", "SSGG"])
+    fpath0 = cfg.get("fpath0", "SVSV")
+
+    def fp(b):
+        if b == B - 1:
+            return cfg.get("fpath7", "SSSS")
+        return fpath0 if b == 0 else fpaths[b % 2]
+
+    wg1 = cfg.get("wg1", "GG")
     wg2 = cfg.get("wg2", "GGGG")
     h0 = cfg.get("h0", "SSSS")
 
@@ -51,46 +59,51 @@ def program(cfg):
         if k < B:
             add((kind, k))
 
-    def f(b, s):
-        add(("F", b, s, fpaths[b % 2][s]))
+    def rd(k):
+        if k < B:
+            add(("RD", k))
+            for s in range(S):
+                if fp(k)[s] == "G":
+                    add(("BR", k, s))
+
+    def bf(b, s):
+        add(("B", b, s, fp(b)[s]))
+        add(("F", b, s, fp(b)[s]))
 
     def finish(b):
         ld("LDA", b + 3); ld("LDX", b + 4)
-        add(("B", b, 0))
+        bf(b, 0)
+        q(0, b + 2)
         add(("SELF", b, 3)); add(("G", b, 3))
         m(b + 1, 0, 1); m(b + 1, 0, 2)
         t(2, b + 1)
-        add(("B", b, 1))
-        f(b, 0)
-        f(b, 1)
+        bf(b, 1)
         add(("ST", b, 0))
-        q(1, b + 1)
-        h(b + 1, 3)
-        add(("B", b, 2))
-        add(("B", b, 3))
-        f(b, 2)
-        f(b, 3)
+        bf(b, 2)
+        bf(b, 3)
         add(("ST", b, 1))
+        rd(b + 1)
 
-    add(("BIAS0",))
-    add(("LDX", 0)); add(("LDW", 0)); add(("LDW", 1)); add(("LDX", 1)); add(("LDA", 0)); add(("LDW", 2))
+    add(("LDX", 0)); add(("LDW", 0)); add(("BIAS0",)); add(("LDW", 1)); add(("LDX", 1)); add(("LDA", 0)); add(("LDW", 2))
     add(("LDA", 1)); add(("LDX", 2)); add(("LDA", 2)); add(("LDX", 3))
-    add(("BIAS",))
     t(0, 0)
     add(("C", 0, 0, 0)); add(("C", 0, 0, 1, "V"))
     add(("WG", 0, "V", 0, 2)); add(("WG", 0, "S", 2, 4))
+    add(("BIAS", 0))
     q(0, 0)
     add(("WQ", 0, 0, 2))
     m(0, 0, 0); m(0, 0, 1)
     add(("WQ", 0, 2, 4))
     m(0, 0, 2)
     add(("WG", 1, wg1[0], 0, 2)); add(("WG", 1, wg1[1], 2, 4))
+    add(("BIAS", 1))
     t(0, 1)
     c(0, 1)
     add(("A", 0, 0, 0)); m(0, 0, 3)
     add(("A", 0, 0, 1))
     add(("A", 0, 0, 2))
     add(("A", 0, 0, 3))
+    add(("H", 0, 0, h0[0]))
     t(1, 0); c(1, 0)
     q(0, 1)
     add(("WQ", 1, 0, 4))
@@ -98,13 +111,14 @@ def program(cfg):
     add(("QM", 0, 0))
     for i in range(4):
         add(("WG", 2, wg2[i], i, i + 1))
+    add(("H", 0, 1, h0[1]))
     t(2, 0); c(2, 0)
     add(("A", 0, 1, 0)); m(0, 1, 3)
-    add(("H", 0, 0, h0[0]))
     add(("A", 0, 1, 1)); m(1, 0, 0)
-    add(("H", 0, 1, h0[1]))
+    add(("H", 0, 2, h0[2]))
     add(("A", 0, 1, 2))
     add(("A", 0, 1, 3))
+    add(("BIAS", 2))
     t(0, 2); c(0, 2)
     q(1, 0)
     add(("WQ", 2, 0, 4))
@@ -112,14 +126,14 @@ def program(cfg):
         add(("SELF", 0, s))
     add(("QM", 0, 1))
     q(2, 0)
-    add(("H", 0, 2, h0[2]))
     add(("H", 0, 3, h0[3]))
     for s in range(3):
         add(("G", 0, s))
     t(1, 1); c(1, 1)
-    q(0, 2)
-    add(("RD", 0))
-    h(1, 0); h(1, 1); h(1, 2)
+    rd(0)
+    h(1, 0); h(1, 1)
+    q(1, 1)
+    h(1, 2); h(1, 3)
     finish(0)
     for b in range(1, B):
         add(("A", b, 0, 0)); m(b, 0, 3)
@@ -128,25 +142,25 @@ def program(cfg):
         add(("A", b, 0, 2)); m(b, 1, 1)
         add(("A", b, 0, 3)); m(b, 1, 2)
         h(b + 1, 0)
+        h(b + 1, 1)
         add(("A", b, 1, 0)); m(b, 1, 3)
-        add(("QM", b, 0))
-        t(0, b + 2)
-        c(0, b + 2)
+        t(1, b + 1)
+        c(1, b + 1)
         add(("A", b, 1, 1)); m(b + 1, 0, 0)
+        add(("QM", b, 0))
         for s in range(3):
             add(("SELF", b, s))
-        h(b + 1, 1)
+        h(b + 1, 2)
         add(("A", b, 1, 2))
-        t(1, b + 1)
+        t(0, b + 2)
         add(("A", b, 1, 3))
         q(2, b)
         add(("QM", b, 1))
-        c(1, b + 1)
+        c(0, b + 2)
         for s in range(3):
             add(("G", b, s))
-        q(0, b + 2)
-        add(("RD", b))
-        h(b + 1, 2)
+        q(1, b + 1)
+        h(b + 1, 3)
         finish(b)
     return ops
 
@@ -206,14 +220,13 @@ def tile_rgcn_layer_pa_t_kernel(tc, x, adj, wr, br, w0, b0, out):
         def op_bias0():
             nc.vector.memset(zb[:], 0.0)
             nc.vector.memset(ones[:], 1.0)
-            nc.scalar.dma_start(out=zb[0:1, 0 : 2 * D], in_=br.rearrange("r d -> (r d)").unsqueeze(0))
-            nc.scalar.dma_start(out=zb[0:1, 2 * D : 3 * D], in_=b0.unsqueeze(0))
+            nc.sync.dma_start(out=zb[0:1, 0 : 2 * D], in_=br.rearrange("r d -> (r d)").unsqueeze(0))
+            nc.sync.dma_start(out=zb[0:1, 2 * D : 3 * D], in_=b0.unsqueeze(0))
 
-        def op_bias():
-            for w in range(3):
-                bank = ps_o.tile([P, D], F32, name="bank_o")
-                nc.tensor.matmul(out=bank[:], lhsT=ones[:], rhs=zb[:, w * D : (w + 1) * D], start=True, stop=True)
-                copy_on("SVS"[w], bias[:, w * D : (w + 1) * D], bank[:])
+        def op_bias(w):
+            bank = ps_o.tile([P, D], F32, name="bank_o")
+            nc.tensor.matmul(out=bank[:], lhsT=ones[:], rhs=zb[:, w * D : (w + 1) * D], start=True, stop=True)
+            nc.scalar.copy(out=bias[:, w * D : (w + 1) * D], in_=bank[:])
 
         def op_wg(w, e, c0, c1):
             cols = slice(c0 * P, c1 * P)
@@ -347,9 +360,31 @@ def tile_rgcn_layer_pa_t_kernel(tc, x, adj, wr, br, w0, b0, out):
                     stop=(r == R - 1),
                 )
 
-        def op_b(b, s):
+        def op_br(b, s):
+            b0r = pool["b6"].tile([P, D], F32, name="b0r")
+            nc.gpsimd.tensor_scalar(
+                out=b0r[:],
+                in0=bias[:, 2 * D : 3 * D],
+                scalar1=tl[("rden", b)][:, s : s + 1],
+                scalar2=0.0,
+                op0=ALU.mult,
+                op1=ALU.add,
+            )
+            tl[("b0r", b, s)] = b0r
+
+        def op_b(b, s, e):
             t = pool["b4"].tile([P, D], F32, name="t")
-            nc.vector.tensor_tensor(out=t[:], in0=tl[("bo", b, s)][:], in1=bias[:, 2 * D : 3 * D], op=ALU.add)
+            if e == "G":
+                nc.vector.scalar_tensor_tensor(
+                    out=t[:],
+                    in0=tl[("bo", b, s)][:],
+                    scalar=tl[("rden", b)][:, s : s + 1],
+                    in1=tl[("b0r", b, s)][:],
+                    op0=ALU.mult,
+                    op1=ALU.add,
+                )
+            else:
+                nc.vector.tensor_tensor(out=t[:], in0=tl[("bo", b, s)][:], in1=bias[:, 2 * D : 3 * D], op=ALU.add)
             tl[("t", b, s)] = t
 
         def op_f(b, s, e):
@@ -359,13 +394,17 @@ def tile_rgcn_layer_pa_t_kernel(tc, x, adj, wr, br, w0, b0, out):
             rd = tl[("rden", b)][:, s : s + 1]
             if e == "S":
                 nc.scalar.activation(out=o_ap, in_=tl[("t", b, s)][:], func=ACT.Relu, scale=rd)
-            else:
+            elif e == "V":
                 nc.vector.tensor_scalar(
                     out=o_ap, in0=tl[("t", b, s)][:], scalar1=rd, scalar2=0.0, op0=ALU.mult, op1=ALU.max
                 )
+            else:
+                nc.gpsimd.tensor_scalar(
+                    out=o_ap, in0=tl[("t", b, s)][:], scalar1=FLT_MAX, scalar2=0.0, op0=ALU.min, op1=ALU.max
+                )
 
         def op_st(b, u):
-            nc.scalar.dma_start(
+            nc.sync.dma_start(
                 out=out[b, 256 * u : 256 * (u + 1), :].rearrange("(p e) d -> p (e d)", e=2),
                 in_=tl[("o", b, u)][:].rearrange("p e d -> p (e d)"),
             )
@@ -373,7 +412,7 @@ def tile_rgcn_layer_pa_t_kernel(tc, x, adj, wr, br, w0, b0, out):
         table = {
             "LDX": op_ldx, "LDA": op_lda, "LDW": op_ldw, "BIAS0": op_bias0, "BIAS": op_bias, "WG": op_wg, "WQ": op_wq, "T": op_t,
             "C": op_c, "Q": op_q, "H": op_h, "RD": op_rd, "M": op_m, "A": op_a, "QM": op_qm, "SELF": op_self,
-            "G": op_g, "B": op_b, "F": op_f, "ST": op_st,
+            "G": op_g, "BR": op_br, "B": op_b, "F": op_f, "ST": op_st,
         }
         for op in program(CFG):
             table[op[0]](*op[1:])

@@ -21,17 +21,14 @@ CFG = {}
 def program(cfg):
     ops = []
     add = ops.append
-    fpaths = cfg.get("fpath", ["SGGG", "SSGG"])
-    fpath0 = cfg.get("fpath0", "SVSV")
+    fpaths = cfg.get("fpath", ["SVSV", "SVSV"])
+    wg2 = cfg.get("wg2", "VVVV")
+    h0 = cfg.get("h0", "SSSS")
 
     def fp(b):
         if b == B - 1:
             return cfg.get("fpath7", "SSSS")
-        return fpath0 if b == 0 else fpaths[b % 2]
-
-    wg1 = cfg.get("wg1", "GG")
-    wg2 = cfg.get("wg2", "GGGG")
-    h0 = cfg.get("h0", "SSSS")
+        return fpaths[b % 2]
 
     def t(unit, k):
         if 0 <= k < B:
@@ -59,90 +56,93 @@ def program(cfg):
         if k < B:
             add((kind, k))
 
-    def rd(k):
-        if k < B:
-            add(("RD", k))
-            for s in range(S):
-                if fp(k)[s] == "G":
-                    add(("BR", k, s))
-
-    def bf(b, s):
-        add(("B", b, s, fp(b)[s]))
-        add(("F", b, s, fp(b)[s]))
-
     def finish(b):
+        p = fp(b)
         ld("LDA", b + 3); ld("LDX", b + 4)
-        bf(b, 0)
-        q(0, b + 2)
+        add(("B", b, 0, p[0]))
+        if b > 0:
+            q(0, b + 2)
         add(("SELF", b, 3)); add(("G", b, 3))
         m(b + 1, 0, 1); m(b + 1, 0, 2)
         t(2, b + 1)
-        bf(b, 1)
+        add(("B", b, 1, p[1]))
+        add(("F", b, 0, p[0]))
+        add(("B", b, 2, p[2]))
+        add(("F", b, 1, p[1]))
         add(("ST", b, 0))
-        bf(b, 2)
-        bf(b, 3)
-        add(("ST", b, 1))
-        rd(b + 1)
+        add(("B", b, 3, p[3]))
+        add(("F", b, 2, p[2]))
+        h(b + 1, 0)
+        if b == 0:
+            q(0, 2)
+        if b == B - 1:
+            last(b)
 
-    add(("LDX", 0)); add(("LDW", 0)); add(("BIAS0",)); add(("LDW", 1)); add(("LDX", 1)); add(("LDA", 0)); add(("LDW", 2))
+    def last(b):
+        add(("F", b, 3, fp(b)[3]))
+        add(("ST", b, 1))
+
+    add(("LDX", 0)); add(("LDW", 0)); add(("BIAS0",)); add(("LDW", 1)); add(("LDA", 0)); add(("LDX", 1)); add(("LDW", 2))
     add(("LDA", 1)); add(("LDX", 2)); add(("LDA", 2)); add(("LDX", 3))
     t(0, 0)
     add(("C", 0, 0, 0)); add(("C", 0, 0, 1, "V"))
     add(("WG", 0, "V", 0, 2)); add(("WG", 0, "S", 2, 4))
-    add(("BIAS", 0))
+    for w in range(3):
+        add(("BIAS", w))
     q(0, 0)
     add(("WQ", 0, 0, 2))
     m(0, 0, 0); m(0, 0, 1)
     add(("WQ", 0, 2, 4))
     m(0, 0, 2)
-    add(("WG", 1, wg1[0], 0, 2)); add(("WG", 1, wg1[1], 2, 4))
-    add(("BIAS", 1))
-    t(0, 1)
-    c(0, 1)
+    add(("WG", 1, "V", 0, 4))
+    t(1, 0)
     add(("A", 0, 0, 0)); m(0, 0, 3)
-    add(("A", 0, 0, 1))
-    add(("A", 0, 0, 2))
-    add(("A", 0, 0, 3))
-    add(("H", 0, 0, h0[0]))
-    t(1, 0); c(1, 0)
-    q(0, 1)
     add(("WQ", 1, 0, 4))
-    m(0, 1, 0); m(0, 1, 1); m(0, 1, 2)
-    add(("QM", 0, 0))
+    add(("H", 0, 0, h0[0]))
+    c(1, 0)
+    add(("A", 0, 0, 1)); m(0, 1, 0)
+    add(("A", 0, 0, 2))
     for i in range(4):
         add(("WG", 2, wg2[i], i, i + 1))
+    t(2, 0)
+    m(0, 1, 1)
+    add(("A", 0, 0, 3)); m(0, 1, 2)
     add(("H", 0, 1, h0[1]))
-    t(2, 0); c(2, 0)
+    c(2, 0)
     add(("A", 0, 1, 0)); m(0, 1, 3)
-    add(("A", 0, 1, 1)); m(1, 0, 0)
-    add(("H", 0, 2, h0[2]))
+    add(("A", 0, 1, 1))
     add(("A", 0, 1, 2))
     add(("A", 0, 1, 3))
-    add(("BIAS", 2))
-    t(0, 2); c(0, 2)
-    q(1, 0)
+    t(0, 1)
+    add(("H", 0, 2, h0[2]))
+    c(0, 1)
+    add(("QM", 0, 0))
     add(("WQ", 2, 0, 4))
+    t(1, 1)
     for s in range(3):
         add(("SELF", 0, s))
-    add(("QM", 0, 1))
+    q(1, 0)
     q(2, 0)
+    add(("QM", 0, 1))
     add(("H", 0, 3, h0[3]))
+    c(1, 1)
     for s in range(3):
         add(("G", 0, s))
-    t(1, 1); c(1, 1)
-    rd(0)
-    h(1, 0); h(1, 1)
+    q(0, 1)
+    m(1, 0, 0)
+    add(("RD", 0))
+    t(0, 2); c(0, 2)
     q(1, 1)
-    h(1, 2); h(1, 3)
     finish(0)
     for b in range(1, B):
         add(("A", b, 0, 0)); m(b, 0, 3)
+        last(b - 1)
         c(2, b)
         add(("A", b, 0, 1)); m(b, 1, 0)
         add(("A", b, 0, 2)); m(b, 1, 1)
         add(("A", b, 0, 3)); m(b, 1, 2)
-        h(b + 1, 0)
-        h(b + 1, 1)
+        h(b, 1)
+        h(b, 2)
         add(("A", b, 1, 0)); m(b, 1, 3)
         t(1, b + 1)
         c(1, b + 1)
@@ -150,7 +150,7 @@ def program(cfg):
         add(("QM", b, 0))
         for s in range(3):
             add(("SELF", b, s))
-        h(b + 1, 2)
+        h(b, 3)
         add(("A", b, 1, 2))
         t(0, b + 2)
         add(("A", b, 1, 3))
@@ -160,7 +160,7 @@ def program(cfg):
         for s in range(3):
             add(("G", b, s))
         q(1, b + 1)
-        h(b + 1, 3)
+        add(("RD", b))
         finish(b)
     return ops
 

@@ -15,7 +15,7 @@ B, R, S = 8, 2, 4
 N, D, P = 512, 512, 128
 FLOPS = 2 * B * (R * N * D * D + N * R * N * D + N * D * D)
 FLT_MAX = 3.4028234663852886e38
-CFG = {}
+CFG = {"fpath":["SSSS","SSSS"]}
 
 
 def program(cfg):
@@ -60,9 +60,7 @@ def program(cfg):
         p = fp(b)
         ld("LDA", b + 3); ld("LDX", b + 4)
         add(("B", b, 0, p[0]))
-        if b > 0:
-            q(0, b + 2)
-        add(("SELF", b, 3)); add(("G", b, 3))
+        add(("SELF", b, 3)); add(("G", b, 3, 0)); add(("G", b, 3, 1))
         m(b + 1, 0, 1); m(b + 1, 0, 2)
         t(2, b + 1)
         add(("B", b, 1, p[1]))
@@ -70,8 +68,12 @@ def program(cfg):
         add(("B", b, 2, p[2]))
         add(("F", b, 1, p[1]))
         add(("ST", b, 0))
+        if b > 0:
+            q(0, b + 2)
         add(("B", b, 3, p[3]))
         add(("F", b, 2, p[2]))
+        if b == B - 1:
+            add(("ST1", b, 2))
         h(b + 1, 0)
         if b == 0:
             q(0, 2)
@@ -80,7 +82,10 @@ def program(cfg):
 
     def last(b):
         add(("F", b, 3, fp(b)[3]))
-        add(("ST", b, 1))
+        if b == B - 1:
+            add(("ST1", b, 3))
+        else:
+            add(("ST", b, 1))
 
     add(("LDX", 0)); add(("LDW", 0)); add(("BIAS0",)); add(("LDW", 1)); add(("LDA", 0)); add(("LDX", 1)); add(("LDW", 2))
     add(("LDA", 1)); add(("LDX", 2)); add(("LDA", 2)); add(("LDX", 3))
@@ -119,15 +124,15 @@ def program(cfg):
     add(("QM", 0, 0))
     add(("WQ", 2, 0, 4))
     t(1, 1)
-    for s in range(3):
-        add(("SELF", 0, s))
     q(1, 0)
+    for s in range(3):
+        add(("SELF", 0, s)); add(("G", 0, s, 0))
     q(2, 0)
     add(("QM", 0, 1))
     add(("H", 0, 3, h0[3]))
     c(1, 1)
     for s in range(3):
-        add(("G", 0, s))
+        add(("G", 0, s, 1))
     q(0, 1)
     m(1, 0, 0)
     add(("RD", 0))
@@ -149,16 +154,16 @@ def program(cfg):
         add(("A", b, 1, 1)); m(b + 1, 0, 0)
         add(("QM", b, 0))
         for s in range(3):
-            add(("SELF", b, s))
+            add(("SELF", b, s)); add(("G", b, s, 0))
         h(b, 3)
         add(("A", b, 1, 2))
-        t(0, b + 2)
         add(("A", b, 1, 3))
         q(2, b)
         add(("QM", b, 1))
-        c(0, b + 2)
         for s in range(3):
-            add(("G", b, s))
+            add(("G", b, s, 1))
+        t(0, b + 2)
+        c(0, b + 2)
         q(1, b + 1)
         add(("RD", b))
         finish(b)
@@ -290,14 +295,16 @@ def tile_rgcn_layer_pa_t_kernel(tc, x, adj, wr, br, w0, b0, out):
                 tl[("dsum", k)] = pool["b3"].tile([P, S], F32, name="dsum")
             junk = pool["b2"].tile([P, R, N], BF16, name="junk")
             nc.scalar.activation(
-                out=junk[:], in_=tl[("a", k)][:, :, s, :], func=ACT.Copy, accum_out=tl[("dsum", k)][:, s : s + 1]
+                out=junk[:],
+                in_=tl[("a", k)][:, :, s, :],
+                func=ACT.Copy,
+                bias=1.0 / (R * N),
+                accum_out=tl[("dsum", k)][:, s : s + 1],
             )
 
         def op_rd(k):
-            den = pool["b3"].tile([P, S], F32, name="den")
-            nc.vector.tensor_scalar_add(den[:], tl[("dsum", k)][:], 1.0)
             rden = pool["b3"].tile([P, S], F32, name="rden")
-            nc.vector.reciprocal(rden[:], den[:])
+            nc.vector.reciprocal(rden[:], tl[("dsum", k)][:])
             tl[("rden", k)] = rden
 
         def op_m(b, r, dc):
@@ -345,20 +352,19 @@ def tile_rgcn_layer_pa_t_kernel(tc, x, adj, wr, br, w0, b0, out):
             )
             tl[("bo", b, s)] = bank
 
-        def op_g(b, s):
+        def op_g(b, s, r):
             rows = slice(s * P, (s + 1) * P)
-            for r in range(R):
-                aw, asc = tl[("q", 1 + r, b)]
-                mw, msc = tl[("qm", b, r)]
-                nc.tensor.matmul_mx(
-                    out=tl[("bo", b, s)][:],
-                    lhsT=aw[:, rows].bitcast(FP8X4),
-                    lhsT_scale=asc[:, rows],
-                    rhs=mw[:].bitcast(FP8X4),
-                    rhs_scale=msc[:],
-                    start=False,
-                    stop=(r == R - 1),
-                )
+            aw, asc = tl[("q", 1 + r, b)]
+            mw, msc = tl[("qm", b, r)]
+            nc.tensor.matmul_mx(
+                out=tl[("bo", b, s)][:],
+                lhsT=aw[:, rows].bitcast(FP8X4),
+                lhsT_scale=asc[:, rows],
+                rhs=mw[:].bitcast(FP8X4),
+                rhs_scale=msc[:],
+                start=False,
+                stop=(r == R - 1),
+            )
 
         def op_br(b, s):
             b0r = pool["b6"].tile([P, D], F32, name="b0r")
@@ -409,10 +415,16 @@ def tile_rgcn_layer_pa_t_kernel(tc, x, adj, wr, br, w0, b0, out):
                 in_=tl[("o", b, u)][:].rearrange("p e d -> p (e d)"),
             )
 
+        def op_st1(b, s):
+            nc.sync.dma_start(
+                out=out[b, 256 * (s // 2) : 256 * (s // 2 + 1), :].rearrange("(p e) d -> p e d", e=2)[:, s % 2, :],
+                in_=tl[("o", b, s // 2)][:, s % 2, :],
+            )
+
         table = {
             "LDX": op_ldx, "LDA": op_lda, "LDW": op_ldw, "BIAS0": op_bias0, "BIAS": op_bias, "WG": op_wg, "WQ": op_wq, "T": op_t,
             "C": op_c, "Q": op_q, "H": op_h, "RD": op_rd, "M": op_m, "A": op_a, "QM": op_qm, "SELF": op_self,
-            "G": op_g, "BR": op_br, "B": op_b, "F": op_f, "ST": op_st,
+            "G": op_g, "BR": op_br, "B": op_b, "F": op_f, "ST": op_st, "ST1": op_st1,
         }
         for op in program(CFG):
             table[op[0]](*op[1:])

@@ -15,7 +15,7 @@ B, R, S = 8, 2, 4
 N, D, P = 512, 512, 128
 FLOPS = 2 * B * (R * N * D * D + N * R * N * D + N * D * D)
 FLT_MAX = 3.4028234663852886e38
-CFG = {"fpath":["SSSS","SSSS"]}
+CFG = {"fpath":["SSSV","SSSV"]}
 
 
 def program(cfg):
@@ -48,18 +48,27 @@ def program(cfg):
         if b < B:
             add(("M", b, r, dc))
 
+    taken = set()
+
     def h(k, s):
-        if 1 <= k < B:
+        if 1 <= k < B and (k, s) not in taken:
+            taken.add((k, s))
             add(("H", k, s, "S"))
 
     def ld(kind, k):
         if k < B:
             add((kind, k))
 
+    def early_a(b):
+        if b < B:
+            add(("A", b, 0, 0))
+
     def finish(b):
         p = fp(b)
         ld("LDA", b + 3); ld("LDX", b + 4)
         add(("B", b, 0, p[0]))
+        if b > 0:
+            add(("RD", b))
         add(("SELF", b, 3)); add(("G", b, 3, 0)); add(("G", b, 3, 1))
         m(b + 1, 0, 1); m(b + 1, 0, 2)
         t(2, b + 1)
@@ -99,7 +108,8 @@ def program(cfg):
     m(0, 0, 0); m(0, 0, 1)
     add(("WQ", 0, 2, 4))
     m(0, 0, 2)
-    add(("WG", 1, "V", 0, 4))
+    for i in range(4):
+        add(("WG", 1, cfg.get("wg1", "VVVV")[i], i, i + 1))
     t(1, 0)
     add(("A", 0, 0, 0)); m(0, 0, 3)
     add(("WQ", 1, 0, 4))
@@ -127,23 +137,26 @@ def program(cfg):
     q(1, 0)
     for s in range(3):
         add(("SELF", 0, s)); add(("G", 0, s, 0))
+    q(0, 1)
+    m(1, 0, 0)
     q(2, 0)
     add(("QM", 0, 1))
     add(("H", 0, 3, h0[3]))
     c(1, 1)
     for s in range(3):
         add(("G", 0, s, 1))
-    q(0, 1)
-    m(1, 0, 0)
     add(("RD", 0))
+    h(1, 0)
+    h(1, 1)
     t(0, 2); c(0, 2)
     q(1, 1)
+    early_a(1)
     finish(0)
     for b in range(1, B):
-        add(("A", b, 0, 0)); m(b, 0, 3)
-        last(b - 1)
+        m(b, 0, 3)
         c(2, b)
         add(("A", b, 0, 1)); m(b, 1, 0)
+        last(b - 1)
         add(("A", b, 0, 2)); m(b, 1, 1)
         add(("A", b, 0, 3)); m(b, 1, 2)
         h(b, 1)
@@ -164,8 +177,8 @@ def program(cfg):
             add(("G", b, s, 1))
         t(0, b + 2)
         c(0, b + 2)
+        early_a(b + 1)
         q(1, b + 1)
-        add(("RD", b))
         finish(b)
     return ops
 

@@ -11,176 +11,12 @@ FP8X4 = mybir.dt.float8_e4m3fn_x4
 ALU = mybir.AluOpType
 ACT = mybir.ActivationFunctionType
 
-B, R, S = 8, 2, 4
-N, D, P = 512, 512, 128
+B, R, N, D = 8, 2, 512, 512
+P = 128
+S = 4
+X, A0, A1 = 0, 1, 2
+W0 = R
 FLOPS = 2 * B * (R * N * D * D + N * R * N * D + N * D * D)
-FLT_MAX = 3.4028234663852886e38
-CFG = {"fpath":["SSSV","SSSV"]}
-
-
-def program(cfg):
-    ops = []
-    add = ops.append
-    fpaths = cfg.get("fpath", ["SVSV", "SVSV"])
-    wg2 = cfg.get("wg2", "VVVV")
-    h0 = cfg.get("h0", "SSSS")
-
-    def fp(b):
-        if b == B - 1:
-            return cfg.get("fpath7", "SSSS")
-        return fpaths[b % 2]
-
-    def t(unit, k):
-        if 0 <= k < B:
-            add(("T", unit, k, 0))
-            add(("T", unit, k, 1))
-
-    def c(unit, k):
-        if 0 <= k < B:
-            add(("C", unit, k, 0))
-            add(("C", unit, k, 1))
-
-    def q(unit, k):
-        if 0 <= k < B:
-            add(("Q", unit, k))
-
-    def m(b, r, dc):
-        if b < B:
-            add(("M", b, r, dc))
-
-    taken = set()
-
-    def h(k, s):
-        if 1 <= k < B and (k, s) not in taken:
-            taken.add((k, s))
-            add(("H", k, s, "S"))
-
-    def ld(kind, k):
-        if k < B:
-            add((kind, k))
-
-    def early_a(b):
-        if b < B:
-            add(("A", b, 0, 0))
-
-    def finish(b):
-        p = fp(b)
-        ld("LDA", b + 3); ld("LDX", b + 4)
-        add(("B", b, 0, p[0]))
-        if b > 0:
-            add(("RD", b))
-        add(("SELF", b, 3)); add(("G", b, 3, 0)); add(("G", b, 3, 1))
-        m(b + 1, 0, 1); m(b + 1, 0, 2)
-        t(2, b + 1)
-        add(("B", b, 1, p[1]))
-        add(("F", b, 0, p[0]))
-        add(("B", b, 2, p[2]))
-        add(("F", b, 1, p[1]))
-        add(("ST", b, 0))
-        if b > 0:
-            q(0, b + 2)
-        add(("B", b, 3, p[3]))
-        add(("F", b, 2, p[2]))
-        if b == B - 1:
-            add(("ST1", b, 2))
-        h(b + 1, 0)
-        if b == 0:
-            q(0, 2)
-        if b == B - 1:
-            last(b)
-
-    def last(b):
-        add(("F", b, 3, fp(b)[3]))
-        if b == B - 1:
-            add(("ST1", b, 3))
-        else:
-            add(("ST", b, 1))
-
-    add(("LDX", 0)); add(("LDW", 0)); add(("BIAS0",)); add(("LDW", 1)); add(("LDA", 0)); add(("LDX", 1)); add(("LDW", 2))
-    add(("LDA", 1)); add(("LDX", 2)); add(("LDA", 2)); add(("LDX", 3))
-    t(0, 0)
-    add(("C", 0, 0, 0)); add(("C", 0, 0, 1, "V"))
-    add(("WG", 0, "V", 0, 2)); add(("WG", 0, "S", 2, 4))
-    for w in range(3):
-        add(("BIAS", w))
-    q(0, 0)
-    add(("WQ", 0, 0, 2))
-    m(0, 0, 0); m(0, 0, 1)
-    add(("WQ", 0, 2, 4))
-    m(0, 0, 2)
-    for i in range(4):
-        add(("WG", 1, cfg.get("wg1", "VVVV")[i], i, i + 1))
-    t(1, 0)
-    add(("A", 0, 0, 0)); m(0, 0, 3)
-    add(("WQ", 1, 0, 4))
-    add(("H", 0, 0, h0[0]))
-    c(1, 0)
-    add(("A", 0, 0, 1)); m(0, 1, 0)
-    add(("A", 0, 0, 2))
-    for i in range(4):
-        add(("WG", 2, wg2[i], i, i + 1))
-    t(2, 0)
-    m(0, 1, 1)
-    add(("A", 0, 0, 3)); m(0, 1, 2)
-    add(("H", 0, 1, h0[1]))
-    c(2, 0)
-    add(("A", 0, 1, 0)); m(0, 1, 3)
-    add(("A", 0, 1, 1))
-    add(("A", 0, 1, 2))
-    add(("A", 0, 1, 3))
-    t(0, 1)
-    add(("H", 0, 2, h0[2]))
-    c(0, 1)
-    add(("QM", 0, 0))
-    add(("WQ", 2, 0, 4))
-    t(1, 1)
-    q(1, 0)
-    for s in range(3):
-        add(("SELF", 0, s)); add(("G", 0, s, 0))
-    q(0, 1)
-    m(1, 0, 0)
-    q(2, 0)
-    add(("QM", 0, 1))
-    add(("H", 0, 3, h0[3]))
-    c(1, 1)
-    for s in range(3):
-        add(("G", 0, s, 1))
-    add(("RD", 0))
-    h(1, 0)
-    h(1, 1)
-    t(0, 2); c(0, 2)
-    q(1, 1)
-    early_a(1)
-    finish(0)
-    for b in range(1, B):
-        m(b, 0, 3)
-        c(2, b)
-        add(("A", b, 0, 1)); m(b, 1, 0)
-        last(b - 1)
-        add(("A", b, 0, 2)); m(b, 1, 1)
-        add(("A", b, 0, 3)); m(b, 1, 2)
-        h(b, 1)
-        h(b, 2)
-        add(("A", b, 1, 0)); m(b, 1, 3)
-        t(1, b + 1)
-        c(1, b + 1)
-        add(("A", b, 1, 1)); m(b + 1, 0, 0)
-        add(("QM", b, 0))
-        for s in range(3):
-            add(("SELF", b, s)); add(("G", b, s, 0))
-        h(b, 3)
-        add(("A", b, 1, 2))
-        add(("A", b, 1, 3))
-        q(2, b)
-        add(("QM", b, 1))
-        for s in range(3):
-            add(("G", b, s, 1))
-        t(0, b + 2)
-        c(0, b + 2)
-        early_a(b + 1)
-        q(1, b + 1)
-        finish(b)
-    return ops
 
 
 def tile_rgcn_layer_pa_t_kernel(tc, x, adj, wr, br, w0, b0, out):
@@ -196,6 +32,7 @@ def tile_rgcn_layer_pa_t_kernel(tc, x, adj, wr, br, w0, b0, out):
         ident = const.tile([P, P], F32, name="ident")
         make_identity(nc, ident[:])
         ctx.enter_context(tc.manual_schedule())
+
         ones = const.tile([P, P], BF16, name="ones")
         zb = const.tile([P, 3 * D], BF16, name="zb")
         bias = const.tile([P, 3 * D], BF16, name="bias")
@@ -204,124 +41,152 @@ def tile_rgcn_layer_pa_t_kernel(tc, x, adj, wr, br, w0, b0, out):
         w_words = const.tile([P, 3 * D], U32, name="w_words", align_bytes=64)
         w_scales = const.tile([P, 3 * D], U8, name="w_scales", align_bytes=64)
 
-        tl = {}
+        live = {}
 
-        def copy_on(e, out_ap, in_ap):
-            if e == "S":
-                nc.scalar.copy(out=out_ap, in_=in_ap)
-            else:
-                nc.vector.tensor_copy(out=out_ap, in_=in_ap)
 
-        def op_ldx(k):
+        def load_x(k):
+            if k >= B:
+                return
             x_sb = pool["b4"].tile([P, S, D], BF16, name="x_sb")
             nc.sync.dma_start(
                 out=x_sb[:].rearrange("p (u e) f -> p u (e f)", u=2),
                 in_=x[k].rearrange("(u p e) f -> p u (e f)", u=2, e=2),
             )
-            tl[("x", k)] = x_sb
+            live[("x", k)] = x_sb
 
-        def op_lda(k):
+        def load_adj(k):
+            if k >= B:
+                return
             a_sb = pool["b4"].tile([P, R, S, N], BF16, name="a_sb")
             nc.sync.dma_start(
                 out=a_sb[:].rearrange("p r (u e) j -> p (r u) (e j)", u=2),
                 in_=adj[k].rearrange("r (u p e) j -> p (r u) (e j)", u=2, e=2),
             )
-            tl[("a", k)] = a_sb
+            live[("a", k)] = a_sb
 
-        def op_ldw(w):
+        def load_weight(w):
             src = wr[w] if w < R else w0
             nc.sync.dma_start(
                 out=w_raw[:, w].rearrange("p (u e) c -> p u (e c)", u=2),
                 in_=src.rearrange("(u p e) c -> p u (e c)", u=2, e=2),
             )
 
-        def op_bias0():
+        def load_bias_rows():
             nc.vector.memset(zb[:], 0.0)
             nc.vector.memset(ones[:], 1.0)
-            nc.sync.dma_start(out=zb[0:1, 0 : 2 * D], in_=br.rearrange("r d -> (r d)").unsqueeze(0))
-            nc.sync.dma_start(out=zb[0:1, 2 * D : 3 * D], in_=b0.unsqueeze(0))
+            nc.sync.dma_start(out=zb[0:1, 0 : R * D], in_=br.rearrange("r d -> (r d)").unsqueeze(0))
+            nc.sync.dma_start(out=zb[0:1, R * D : 3 * D], in_=b0.unsqueeze(0))
 
-        def op_bias(w):
+        def store_pair(b, u):
+            nc.sync.dma_start(
+                out=out[b, 256 * u : 256 * (u + 1), :].rearrange("(p e) d -> p (e d)", e=2),
+                in_=live[("o", b, u)][:].rearrange("p e d -> p (e d)"),
+            )
+
+        def store_slot(b, s):
+            nc.sync.dma_start(
+                out=out[b, 256 * (s // 2) : 256 * (s // 2 + 1), :].rearrange("(p e) d -> p e d", e=2)[:, s % 2, :],
+                in_=live[("o", b, s // 2)][:, s % 2, :],
+            )
+
+
+        def copy_on(engine, out_ap, in_ap):
+            if engine == "scalar":
+                nc.scalar.copy(out=out_ap, in_=in_ap)
+            else:
+                nc.vector.tensor_copy(out=out_ap, in_=in_ap)
+
+        def spread_bias(w):
             bank = ps_o.tile([P, D], F32, name="bank_o")
             nc.tensor.matmul(out=bank[:], lhsT=ones[:], rhs=zb[:, w * D : (w + 1) * D], start=True, stop=True)
             nc.scalar.copy(out=bias[:, w * D : (w + 1) * D], in_=bank[:])
 
-        def op_wg(w, e, c0, c1):
-            cols = slice(c0 * P, c1 * P)
-            if e == "G":
-                nc.gpsimd.tensor_scalar(
-                    out=w_grp[:, w, cols, :],
-                    in0=w_raw[:, w, :, cols].rearrange("p t c -> p c t"),
-                    scalar1=1.0,
-                    scalar2=0.0,
-                    op0=ALU.mult,
-                    op1=ALU.add,
-                )
-            else:
-                copy_on(
-                    e,
-                    w_grp[:, w, cols, :].rearrange("p (c i) t -> p c t i", i=4),
-                    w_raw[:, w, :, cols].rearrange("p t (c i) -> p c t i", i=4),
-                )
-
-        def op_wq(w, c0, c1):
-            cols = slice(w * D + c0 * P, w * D + c1 * P)
-            nc.vector.quantize_mx(
-                out=w_words[:, cols].bitcast(FP8X4),
-                scales=w_scales[:, cols],
-                in_=w_grp[:, w, c0 * P : c1 * P, :].rearrange("p c t -> p (c t)"),
+        def regroup_weight(w, engine, c0, c1):
+            copy_on(
+                engine,
+                w_grp[:, w, c0:c1, :].rearrange("p (c i) t -> p c t i", i=4),
+                w_raw[:, w, :, c0:c1].rearrange("p t (c i) -> p c t i", i=4),
             )
 
-        def op_t(u, k, h):
-            if u == 0:
-                src = tl[("x", k)][:].bitcast(F32)
+        def quantise_weight(w, c0, c1):
+            nc.vector.quantize_mx(
+                out=w_words[:, w * D + c0 : w * D + c1].bitcast(FP8X4),
+                scales=w_scales[:, w * D + c0 : w * D + c1],
+                in_=w_grp[:, w, c0:c1, :].rearrange("p c t -> p (c t)"),
+            )
+
+
+        def transpose_half(m, k, h):
+            if m == X:
+                words = live[("x", k)][:].bitcast(F32)
             else:
-                src = tl[("a", k)][:].bitcast(F32)[:, u - 1]
+                words = live[("a", k)][:].bitcast(F32)[:, m - 1]
             bank = ps_t.tile([P, 2, 256], F32, name="bank_t")
             for sl in range(2):
-                for w in range(2):
+                for u in range(2):
                     nc.tensor.transpose(
-                        bank[:, w, sl * P : (sl + 1) * P], src[:, 2 * h + sl, w * P : (w + 1) * P], ident[:]
+                        bank[:, u, sl * P : (sl + 1) * P], words[:, 2 * h + sl, u * P : (u + 1) * P], ident[:]
                     )
-            tl[("bt", u, k, h)] = bank
+            live[("bt", m, k, h)] = bank
 
-        def op_c(u, k, h, e="S"):
+        def transposes(m, k):
+            if k < B:
+                transpose_half(m, k, 0)
+                transpose_half(m, k, 1)
+
+        def copy_half(m, k, h, engine):
             if h == 0:
-                tl[("g", u, k)] = pool["b2"].tile([P, 512, 2], F32, name="g%d" % u, align_bytes=64)
-            g = tl[("g", u, k)]
-            copy_on(e, g[:, h * 256 : (h + 1) * 256, :], tl[("bt", u, k, h)][:].rearrange("p w c -> p c w"))
-
-        def quantise(g_bf16, tag, bufs):
-            words = pool[bufs].tile([P, 512], U32, name="w_" + tag, align_bytes=64)
-            scales = pool[bufs].tile([P, 512], U8, name="s_" + tag, align_bytes=64)
-            nc.vector.quantize_mx(out=words[:].bitcast(FP8X4), scales=scales[:], in_=g_bf16)
-            return words, scales
-
-        def op_q(u, k):
-            g = tl[("g", u, k)]
-            tl[("q", u, k)] = quantise(
-                g[:].rearrange("p c w -> p (c w)").bitcast(BF16), "q%d" % u, "b3" if u == 0 else "b2"
+                live[("g", m, k)] = pool["b2"].tile([P, 512, 2], F32, name="g%d" % m, align_bytes=64)
+            copy_on(
+                engine,
+                live[("g", m, k)][:, h * 256 : (h + 1) * 256, :],
+                live[("bt", m, k, h)][:].rearrange("p w c -> p c w"),
             )
 
-        def op_h(k, s, e):
-            if ("dsum", k) not in tl:
-                tl[("dsum", k)] = pool["b3"].tile([P, S], F32, name="dsum")
+        def copies(m, k):
+            if k < B:
+                copy_half(m, k, 0, "scalar")
+                copy_half(m, k, 1, "scalar")
+
+        def quantise_tile(grouped, tag, depth):
+            words = pool[depth].tile([P, 512], U32, name="w_" + tag, align_bytes=64)
+            scales = pool[depth].tile([P, 512], U8, name="s_" + tag, align_bytes=64)
+            nc.vector.quantize_mx(out=words[:].bitcast(FP8X4), scales=scales[:], in_=grouped)
+            return words, scales
+
+        def quantise(m, k):
+            if k < B:
+                live[("q", m, k)] = quantise_tile(
+                    live[("g", m, k)][:].rearrange("p c w -> p (c w)").bitcast(BF16),
+                    "q%d" % m,
+                    "b3" if m == X else "b2",
+                )
+
+
+        def row_sum(k, s):
+            if k >= B:
+                return
+            if ("dsum", k) not in live:
+                live[("dsum", k)] = pool["b3"].tile([P, S], F32, name="dsum")
             junk = pool["b2"].tile([P, R, N], BF16, name="junk")
             nc.scalar.activation(
                 out=junk[:],
-                in_=tl[("a", k)][:, :, s, :],
+                in_=live[("a", k)][:, :, s, :],
                 func=ACT.Copy,
                 bias=1.0 / (R * N),
-                accum_out=tl[("dsum", k)][:, s : s + 1],
+                accum_out=live[("dsum", k)][:, s : s + 1],
             )
 
-        def op_rd(k):
+        def reciprocal_den(k):
             rden = pool["b3"].tile([P, S], F32, name="rden")
-            nc.vector.reciprocal(rden[:], tl[("dsum", k)][:])
-            tl[("rden", k)] = rden
+            nc.vector.reciprocal(rden[:], live[("dsum", k)][:])
+            live[("rden", k)] = rden
 
-        def op_m(b, r, dc):
-            xw, xs = tl[("q", 0, b)]
+
+        def message_passes(b, r, dc):
+            if b >= B:
+                return
+            xw, xs = live[("q", X, b)]
             bank = ps_m.tile([P, S, P], F32, name="bank_m")
             cols = slice(r * D + dc * P, r * D + (dc + 1) * P)
             for s in range(S):
@@ -334,43 +199,46 @@ def tile_rgcn_layer_pa_t_kernel(tc, x, adj, wr, br, w0, b0, out):
                     start=True,
                     stop=True,
                 )
-            tl[("bm", b, r, dc)] = bank
+            live[("bm", b, r, dc)] = bank
 
-        def op_a(b, r, dc):
+        def message_add(b, r, dc):
+            if b >= B:
+                return
             if dc == 0:
-                tl[("mg", b, r)] = pool["b2"].tile([P, D, S], BF16, name="mg", align_bytes=64)
+                live[("mg", b, r)] = pool["b2"].tile([P, D, S], BF16, name="mg", align_bytes=64)
             cols = slice(r * D + dc * P, r * D + (dc + 1) * P)
             nc.vector.tensor_tensor(
-                out=tl[("mg", b, r)][:, dc * P : (dc + 1) * P, :],
-                in0=tl[("bm", b, r, dc)][:].rearrange("p s d -> p d s"),
+                out=live[("mg", b, r)][:, dc * P : (dc + 1) * P, :],
+                in0=live[("bm", b, r, dc)][:].rearrange("p s d -> p d s"),
                 in1=bias[:, cols].unsqueeze(2).to_broadcast([P, P, S]),
                 op=ALU.add,
             )
 
-        def op_qm(b, r):
-            tl[("qm", b, r)] = quantise(tl[("mg", b, r)][:].rearrange("p d s -> p (d s)"), "qm%d" % r, "b2")
+        def quantise_messages(b, r):
+            live[("qm", b, r)] = quantise_tile(live[("mg", b, r)][:].rearrange("p d s -> p (d s)"), "qm%d" % r, "b2")
 
-        def op_self(b, s):
-            xw, xs = tl[("q", 0, b)]
+
+        def self_pass(b, s):
+            xw, xs = live[("q", X, b)]
             rows = slice(s * P, (s + 1) * P)
             bank = ps_o.tile([P, D], F32, name="bank_o")
             nc.tensor.matmul_mx(
                 out=bank[:],
                 lhsT=xw[:, rows].bitcast(FP8X4),
                 lhsT_scale=xs[:, rows],
-                rhs=w_words[:, 2 * D : 3 * D].bitcast(FP8X4),
-                rhs_scale=w_scales[:, 2 * D : 3 * D],
+                rhs=w_words[:, W0 * D : (W0 + 1) * D].bitcast(FP8X4),
+                rhs_scale=w_scales[:, W0 * D : (W0 + 1) * D],
                 start=True,
                 stop=False,
             )
-            tl[("bo", b, s)] = bank
+            live[("bo", b, s)] = bank
 
-        def op_g(b, s, r):
+        def aggregate_pass(b, s, r):
             rows = slice(s * P, (s + 1) * P)
-            aw, asc = tl[("q", 1 + r, b)]
-            mw, msc = tl[("qm", b, r)]
+            aw, asc = live[("q", A0 + r, b)]
+            mw, msc = live[("qm", b, r)]
             nc.tensor.matmul_mx(
-                out=tl[("bo", b, s)][:],
+                out=live[("bo", b, s)][:],
                 lhsT=aw[:, rows].bitcast(FP8X4),
                 lhsT_scale=asc[:, rows],
                 rhs=mw[:].bitcast(FP8X4),
@@ -379,65 +247,167 @@ def tile_rgcn_layer_pa_t_kernel(tc, x, adj, wr, br, w0, b0, out):
                 stop=(r == R - 1),
             )
 
-        def op_br(b, s):
-            b0r = pool["b6"].tile([P, D], F32, name="b0r")
-            nc.gpsimd.tensor_scalar(
-                out=b0r[:],
-                in0=bias[:, 2 * D : 3 * D],
-                scalar1=tl[("rden", b)][:, s : s + 1],
-                scalar2=0.0,
-                op0=ALU.mult,
-                op1=ALU.add,
-            )
-            tl[("b0r", b, s)] = b0r
-
-        def op_b(b, s, e):
+        def output_add(b, s):
             t = pool["b4"].tile([P, D], F32, name="t")
-            if e == "G":
-                nc.vector.scalar_tensor_tensor(
-                    out=t[:],
-                    in0=tl[("bo", b, s)][:],
-                    scalar=tl[("rden", b)][:, s : s + 1],
-                    in1=tl[("b0r", b, s)][:],
-                    op0=ALU.mult,
-                    op1=ALU.add,
-                )
-            else:
-                nc.vector.tensor_tensor(out=t[:], in0=tl[("bo", b, s)][:], in1=bias[:, 2 * D : 3 * D], op=ALU.add)
-            tl[("t", b, s)] = t
+            nc.vector.tensor_tensor(
+                out=t[:], in0=live[("bo", b, s)][:], in1=bias[:, W0 * D : (W0 + 1) * D], op=ALU.add
+            )
+            live[("t", b, s)] = t
 
-        def op_f(b, s, e):
-            if ("o", b, s // 2) not in tl:
-                tl[("o", b, s // 2)] = pool["b6"].tile([P, 2, D], F32, name="o_sb")
-            o_ap = tl[("o", b, s // 2)][:, s % 2, :]
-            rd = tl[("rden", b)][:, s : s + 1]
-            if e == "S":
-                nc.scalar.activation(out=o_ap, in_=tl[("t", b, s)][:], func=ACT.Relu, scale=rd)
-            elif e == "V":
+        def output_scale_relu(b, s):
+            if ("o", b, s // 2) not in live:
+                live[("o", b, s // 2)] = pool["b6"].tile([P, 2, D], F32, name="o_sb")
+            o_ap = live[("o", b, s // 2)][:, s % 2, :]
+            rd = live[("rden", b)][:, s : s + 1]
+            if s < S - 1 or b == B - 1:
+                nc.scalar.activation(out=o_ap, in_=live[("t", b, s)][:], func=ACT.Relu, scale=rd)
+            else:
                 nc.vector.tensor_scalar(
-                    out=o_ap, in0=tl[("t", b, s)][:], scalar1=rd, scalar2=0.0, op0=ALU.mult, op1=ALU.max
+                    out=o_ap, in0=live[("t", b, s)][:], scalar1=rd, scalar2=0.0, op0=ALU.mult, op1=ALU.max
                 )
+
+        def finish(b):
+            load_adj(b + 3)
+            load_x(b + 4)
+            output_add(b, 0)
+            if b > 0:
+                reciprocal_den(b)
+            self_pass(b, 3)
+            aggregate_pass(b, 3, 0)
+            aggregate_pass(b, 3, 1)
+            message_passes(b + 1, 0, 1)
+            message_passes(b + 1, 0, 2)
+            transposes(A1, b + 1)
+            output_add(b, 1)
+            output_scale_relu(b, 0)
+            output_add(b, 2)
+            output_scale_relu(b, 1)
+            store_pair(b, 0)
+            if b > 0:
+                quantise(X, b + 2)
+            output_add(b, 3)
+            output_scale_relu(b, 2)
+            if b == B - 1:
+                store_slot(b, 2)
+            if b > 0:
+                row_sum(b + 1, 0)
             else:
-                nc.gpsimd.tensor_scalar(
-                    out=o_ap, in0=tl[("t", b, s)][:], scalar1=FLT_MAX, scalar2=0.0, op0=ALU.min, op1=ALU.max
-                )
+                quantise(X, 2)
+            if b == B - 1:
+                finish_last_slot(b)
 
-        def op_st(b, u):
-            nc.sync.dma_start(
-                out=out[b, 256 * u : 256 * (u + 1), :].rearrange("(p e) d -> p (e d)", e=2),
-                in_=tl[("o", b, u)][:].rearrange("p e d -> p (e d)"),
-            )
+        def finish_last_slot(b):
+            output_scale_relu(b, 3)
+            if b == B - 1:
+                store_slot(b, 3)
+            else:
+                store_pair(b, 1)
 
-        def op_st1(b, s):
-            nc.sync.dma_start(
-                out=out[b, 256 * (s // 2) : 256 * (s // 2 + 1), :].rearrange("(p e) d -> p e d", e=2)[:, s % 2, :],
-                in_=tl[("o", b, s // 2)][:, s % 2, :],
-            )
+        load_x(0)
+        load_weight(0)
+        load_bias_rows()
+        load_weight(1)
+        load_adj(0)
+        load_x(1)
+        load_weight(W0)
+        load_adj(1)
+        load_x(2)
+        load_adj(2)
+        load_x(3)
+        transposes(X, 0)
+        copy_half(X, 0, 0, "scalar")
+        copy_half(X, 0, 1, "vector")
+        regroup_weight(0, "vector", 0, D // 2)
+        regroup_weight(0, "scalar", D // 2, D)
+        for w in range(3):
+            spread_bias(w)
+        quantise(X, 0)
+        quantise_weight(0, 0, D // 2)
+        message_passes(0, 0, 0)
+        message_passes(0, 0, 1)
+        quantise_weight(0, D // 2, D)
+        message_passes(0, 0, 2)
+        regroup_weight(1, "vector", 0, D)
+        transposes(A0, 0)
+        message_add(0, 0, 0)
+        message_passes(0, 0, 3)
+        quantise_weight(1, 0, D)
+        row_sum(0, 0)
+        copies(A0, 0)
+        message_add(0, 0, 1)
+        message_passes(0, 1, 0)
+        message_add(0, 0, 2)
+        regroup_weight(W0, "vector", 0, D)
+        transposes(A1, 0)
+        message_passes(0, 1, 1)
+        message_add(0, 0, 3)
+        message_passes(0, 1, 2)
+        row_sum(0, 1)
+        copies(A1, 0)
+        message_add(0, 1, 0)
+        message_passes(0, 1, 3)
+        message_add(0, 1, 1)
+        message_add(0, 1, 2)
+        message_add(0, 1, 3)
+        transposes(X, 1)
+        row_sum(0, 2)
+        copies(X, 1)
+        quantise_messages(0, 0)
+        quantise_weight(W0, 0, D)
+        transposes(A0, 1)
+        quantise(A0, 0)
+        for s in range(3):
+            self_pass(0, s)
+            aggregate_pass(0, s, 0)
+        quantise(X, 1)
+        message_passes(1, 0, 0)
+        quantise(A1, 0)
+        quantise_messages(0, 1)
+        row_sum(0, 3)
+        copies(A0, 1)
+        for s in range(3):
+            aggregate_pass(0, s, 1)
+        reciprocal_den(0)
+        row_sum(1, 0)
+        row_sum(1, 1)
+        transposes(X, 2)
+        copies(X, 2)
+        quantise(A0, 1)
+        message_add(1, 0, 0)
+        finish(0)
 
-        table = {
-            "LDX": op_ldx, "LDA": op_lda, "LDW": op_ldw, "BIAS0": op_bias0, "BIAS": op_bias, "WG": op_wg, "WQ": op_wq, "T": op_t,
-            "C": op_c, "Q": op_q, "H": op_h, "RD": op_rd, "M": op_m, "A": op_a, "QM": op_qm, "SELF": op_self,
-            "G": op_g, "BR": op_br, "B": op_b, "F": op_f, "ST": op_st, "ST1": op_st1,
-        }
-        for op in program(CFG):
-            table[op[0]](*op[1:])
+        for b in range(1, B):
+            message_passes(b, 0, 3)
+            copies(A1, b)
+            message_add(b, 0, 1)
+            message_passes(b, 1, 0)
+            finish_last_slot(b - 1)
+            message_add(b, 0, 2)
+            message_passes(b, 1, 1)
+            message_add(b, 0, 3)
+            message_passes(b, 1, 2)
+            if b > 1:
+                row_sum(b, 1)
+            row_sum(b, 2)
+            message_add(b, 1, 0)
+            message_passes(b, 1, 3)
+            transposes(A0, b + 1)
+            copies(A0, b + 1)
+            message_add(b, 1, 1)
+            message_passes(b + 1, 0, 0)
+            quantise_messages(b, 0)
+            for s in range(3):
+                self_pass(b, s)
+                aggregate_pass(b, s, 0)
+            row_sum(b, 3)
+            message_add(b, 1, 2)
+            message_add(b, 1, 3)
+            quantise(A1, b)
+            quantise_messages(b, 1)
+            for s in range(3):
+                aggregate_pass(b, s, 1)
+            transposes(X, b + 2)
+            copies(X, b + 2)
+            message_add(b + 1, 0, 0)
+            quantise(A0, b + 1)
+            finish(b)

@@ -34,6 +34,7 @@ def tile_rgcn_layer_pa_t_kernel(tc, x, adj, wr, br, w0, b0, out):
         ctx.enter_context(tc.manual_schedule())
 
         ones = const.tile([P, P], BF16, name="ones")
+        share = const.tile([P, 1], BF16, name="share")
         zb = const.tile([P, 3 * D], BF16, name="zb")
         bias = const.tile([P, 3 * D], BF16, name="bias")
         w_raw = const.tile([P, 3, S, D], BF16, name="w_raw")
@@ -53,6 +54,15 @@ def tile_rgcn_layer_pa_t_kernel(tc, x, adj, wr, br, w0, b0, out):
                 in_=x[k].rearrange("(u p e) f -> p u (e f)", u=2, e=2),
             )
             live[("x", k)] = x_sb
+
+        def load_first_x():
+            x_sb = pool["b4"].tile([P, S, D], BF16, name="x_sb")
+            for u in range(2):
+                nc.sync.dma_start(
+                    out=x_sb[:, 2 * u : 2 * u + 2, :].rearrange("p e f -> p (e f)"),
+                    in_=x[0, 256 * u : 256 * (u + 1), :].rearrange("(p e) f -> p (e f)", e=2),
+                )
+            live[("x", 0)] = x_sb
 
         def load_adj(k):
             if k >= B:
@@ -74,6 +84,7 @@ def tile_rgcn_layer_pa_t_kernel(tc, x, adj, wr, br, w0, b0, out):
         def load_bias_rows():
             nc.vector.memset(zb[:], 0.0)
             nc.vector.memset(ones[:], 1.0)
+            nc.vector.memset(share[:], 1.0 / P)
             nc.sync.dma_start(out=zb[0:1, 0 : R * D], in_=br.rearrange("r d -> (r d)").unsqueeze(0))
             nc.sync.dma_start(out=zb[0:1, R * D : 3 * D], in_=b0.unsqueeze(0))
 
@@ -163,24 +174,56 @@ def tile_rgcn_layer_pa_t_kernel(tc, x, adj, wr, br, w0, b0, out):
                 )
 
 
-        def row_sum(k, s):
-            if k >= B:
+        def first_tensor_slot(b):
+            return 0 if b == 0 else S - 1
+
+        def den_tile(b):
+            if ("dsum", b) not in live:
+                live[("dsum", b)] = pool["b3"].tile([P, S], F32, name="dsum")
+            return live[("dsum", b)]
+
+        def row_sum(b, s):
+            if s >= first_tensor_slot(b):
                 return
-            if ("dsum", k) not in live:
-                live[("dsum", k)] = pool["b3"].tile([P, S], F32, name="dsum")
             junk = pool["b2"].tile([P, R, N], BF16, name="junk")
             nc.scalar.activation(
                 out=junk[:],
-                in_=live[("a", k)][:, :, s, :],
+                in_=live[("a", b)][:, :, s, :],
                 func=ACT.Copy,
                 bias=1.0 / (R * N),
-                accum_out=live[("dsum", k)][:, s : s + 1],
+                accum_out=den_tile(b)[:, s : s + 1],
             )
 
-        def reciprocal_den(k):
+        def den_passes(b, s):
+            if s < first_tensor_slot(b):
+                return
+            if ("den", b) not in live:
+                if b < B - 1:
+                    live[("den", b)] = ps_o.tile([P, S], F32, name="bank_o")
+                else:
+                    live[("den", b)] = ps_t.tile([P, S], F32, name="bank_t")
+            bank = live[("den", b)]
+            for r in range(R):
+                nodes = live[("g", A0 + r, b)][:].rearrange("p c w -> p (c w)").bitcast(BF16)
+                nodes = nodes.rearrange("p (c t) -> p c t", t=S)
+                for t in range(S):
+                    nc.tensor.matmul(
+                        out=bank[:, s : s + 1],
+                        lhsT=nodes[:, s * P : (s + 1) * P, t],
+                        rhs=ones[:, 0:1],
+                        start=(r == 0 and t == 0),
+                        stop=False,
+                    )
+            nc.tensor.matmul(out=bank[:, s : s + 1], lhsT=ones[:], rhs=share[:], start=False, stop=True)
+
+        def den_copy(b):
+            s0 = first_tensor_slot(b)
+            nc.scalar.copy(out=den_tile(b)[:, s0:S], in_=live[("den", b)][:, s0:S])
+
+        def reciprocal_den(b):
             rden = pool["b3"].tile([P, S], F32, name="rden")
-            nc.vector.reciprocal(rden[:], live[("dsum", k)][:])
-            live[("rden", k)] = rden
+            nc.vector.reciprocal(rden[:], live[("dsum", b)][:])
+            live[("rden", b)] = rden
 
 
         def message_passes(b, r, dc):
@@ -221,7 +264,10 @@ def tile_rgcn_layer_pa_t_kernel(tc, x, adj, wr, br, w0, b0, out):
         def self_pass(b, s):
             xw, xs = live[("q", X, b)]
             rows = slice(s * P, (s + 1) * P)
-            bank = ps_o.tile([P, D], F32, name="bank_o")
+            if s < S - 1 or b < B - 1:
+                bank = ps_o.tile([P, D], F32, name="bank_o")
+            else:
+                bank = ps_t.tile([P, D], F32, name="bank_t")
             nc.tensor.matmul_mx(
                 out=bank[:],
                 lhsT=xw[:, rows].bitcast(FP8X4),
@@ -248,7 +294,7 @@ def tile_rgcn_layer_pa_t_kernel(tc, x, adj, wr, br, w0, b0, out):
             )
 
         def output_add(b, s):
-            t = pool["b4"].tile([P, D], F32, name="t")
+            t = pool["b6"].tile([P, D], F32, name="t")
             nc.vector.tensor_tensor(
                 out=t[:], in0=live[("bo", b, s)][:], in1=bias[:, W0 * D : (W0 + 1) * D], op=ALU.add
             )
@@ -259,57 +305,59 @@ def tile_rgcn_layer_pa_t_kernel(tc, x, adj, wr, br, w0, b0, out):
                 live[("o", b, s // 2)] = pool["b6"].tile([P, 2, D], F32, name="o_sb")
             o_ap = live[("o", b, s // 2)][:, s % 2, :]
             rd = live[("rden", b)][:, s : s + 1]
-            if s < S - 1 or b == B - 1:
-                nc.scalar.activation(out=o_ap, in_=live[("t", b, s)][:], func=ACT.Relu, scale=rd)
-            else:
+            if b == B - 1 and s == S - 1:
                 nc.vector.tensor_scalar(
                     out=o_ap, in0=live[("t", b, s)][:], scalar1=rd, scalar2=0.0, op0=ALU.mult, op1=ALU.max
                 )
+            else:
+                nc.scalar.activation(out=o_ap, in_=live[("t", b, s)][:], func=ACT.Relu, scale=rd)
 
         def finish(b):
             load_adj(b + 3)
             load_x(b + 4)
             output_add(b, 0)
-            if b > 0:
-                reciprocal_den(b)
-            self_pass(b, 3)
-            aggregate_pass(b, 3, 0)
-            aggregate_pass(b, 3, 1)
-            message_passes(b + 1, 0, 1)
-            message_passes(b + 1, 0, 2)
-            transposes(A1, b + 1)
-            output_add(b, 1)
-            output_scale_relu(b, 0)
-            output_add(b, 2)
-            output_scale_relu(b, 1)
-            store_pair(b, 0)
-            if b > 0:
-                quantise(X, b + 2)
-            output_add(b, 3)
-            output_scale_relu(b, 2)
-            if b == B - 1:
-                store_slot(b, 2)
-            if b > 0:
+            if b < B - 1:
+                self_pass(b, 3)
+                aggregate_pass(b, 3, 0)
+                aggregate_pass(b, 3, 1)
+            transposes(X, b + 2)
+            copies(X, b + 2)
+            if b < B - 1:
+                row_sum(b, 2)
+            if b == B - 2:
                 row_sum(b + 1, 0)
-            else:
-                quantise(X, 2)
+                row_sum(b + 1, 1)
             if b == B - 1:
-                finish_last_slot(b)
-
-        def finish_last_slot(b):
-            output_scale_relu(b, 3)
+                reciprocal_den(b)
+                output_scale_relu(b, 0)
+            output_add(b, 1)
             if b == B - 1:
+                output_scale_relu(b, 1)
+                store_pair(b, 0)
+            output_add(b, 2)
+            if b == B - 1:
+                output_scale_relu(b, 2)
+                store_slot(b, 2)
+            message_add(b + 1, 0, 1)
+            output_add(b, 3)
+            message_add(b + 1, 0, 2)
+            quantise(X, b + 2)
+            if b == B - 1:
+                output_scale_relu(b, 3)
                 store_slot(b, 3)
-            else:
-                store_pair(b, 1)
 
-        load_x(0)
+        def scale_and_store(b, u):
+            output_scale_relu(b, 2 * u)
+            output_scale_relu(b, 2 * u + 1)
+            store_pair(b, u)
+
+        load_first_x()
         load_weight(0)
         load_bias_rows()
         load_weight(1)
         load_adj(0)
-        load_x(1)
         load_weight(W0)
+        load_x(1)
         load_adj(1)
         load_x(2)
         load_adj(2)
@@ -319,95 +367,115 @@ def tile_rgcn_layer_pa_t_kernel(tc, x, adj, wr, br, w0, b0, out):
         copy_half(X, 0, 1, "vector")
         regroup_weight(0, "vector", 0, D // 2)
         regroup_weight(0, "scalar", D // 2, D)
-        for w in range(3):
-            spread_bias(w)
+        spread_bias(0)
         quantise(X, 0)
         quantise_weight(0, 0, D // 2)
         message_passes(0, 0, 0)
         message_passes(0, 0, 1)
         quantise_weight(0, D // 2, D)
         message_passes(0, 0, 2)
-        regroup_weight(1, "vector", 0, D)
+        regroup_weight(1, "scalar", 0, D)
+        spread_bias(1)
+        spread_bias(W0)
         transposes(A0, 0)
         message_add(0, 0, 0)
         message_passes(0, 0, 3)
-        quantise_weight(1, 0, D)
-        row_sum(0, 0)
-        copies(A0, 0)
         message_add(0, 0, 1)
-        message_passes(0, 1, 0)
         message_add(0, 0, 2)
-        regroup_weight(W0, "vector", 0, D)
-        transposes(A1, 0)
+        quantise_weight(1, 0, D)
+        message_passes(0, 1, 0)
         message_passes(0, 1, 1)
+        copies(A0, 0)
+        transposes(A1, 0)
         message_add(0, 0, 3)
         message_passes(0, 1, 2)
-        row_sum(0, 1)
+        regroup_weight(W0, "scalar", 0, D)
         copies(A1, 0)
         message_add(0, 1, 0)
         message_passes(0, 1, 3)
         message_add(0, 1, 1)
-        message_add(0, 1, 2)
-        message_add(0, 1, 3)
         transposes(X, 1)
-        row_sum(0, 2)
         copies(X, 1)
-        quantise_messages(0, 0)
-        quantise_weight(W0, 0, D)
-        transposes(A0, 1)
         quantise(A0, 0)
+        message_add(0, 1, 2)
+        quantise_weight(W0, 0, D)
         for s in range(3):
             self_pass(0, s)
+        message_add(0, 1, 3)
+        quantise_messages(0, 0)
+        for s in range(3):
             aggregate_pass(0, s, 0)
-        quantise(X, 1)
-        message_passes(1, 0, 0)
         quantise(A1, 0)
         quantise_messages(0, 1)
-        row_sum(0, 3)
-        copies(A0, 1)
         for s in range(3):
             aggregate_pass(0, s, 1)
-        reciprocal_den(0)
-        row_sum(1, 0)
-        row_sum(1, 1)
+        quantise(X, 1)
+        message_passes(1, 0, 0)
+        load_adj(3)
+        load_x(4)
+        output_add(0, 0)
+        self_pass(0, 3)
+        aggregate_pass(0, 3, 0)
+        aggregate_pass(0, 3, 1)
+        transposes(A0, 1)
+        copies(A0, 1)
+        output_add(0, 1)
+        message_passes(1, 0, 1)
+        message_add(1, 0, 0)
+        message_passes(1, 0, 2)
+        output_add(0, 2)
         transposes(X, 2)
         copies(X, 2)
-        quantise(A0, 1)
-        message_add(1, 0, 0)
-        finish(0)
+        output_add(0, 3)
+        message_add(1, 0, 1)
+        message_add(1, 0, 2)
 
         for b in range(1, B):
             message_passes(b, 0, 3)
-            copies(A1, b)
-            message_add(b, 0, 1)
             message_passes(b, 1, 0)
-            finish_last_slot(b - 1)
-            message_add(b, 0, 2)
             message_passes(b, 1, 1)
+            if b == 1:
+                quantise(A0, 1)
+            transposes(A1, b)
+            copies(A1, b)
             message_add(b, 0, 3)
             message_passes(b, 1, 2)
-            if b > 1:
-                row_sum(b, 1)
-            row_sum(b, 2)
+            for s in range(S):
+                den_passes(b - 1, s)
+            den_copy(b - 1)
+            if b < B - 1:
+                row_sum(b, 0)
+            else:
+                row_sum(b, 2)
             message_add(b, 1, 0)
+            if b == 1:
+                quantise(X, 2)
             message_passes(b, 1, 3)
+            for s in range(3 if b < B - 1 else 4):
+                self_pass(b, s)
+            if b == B - 1:
+                den_passes(b, 3)
+                den_copy(b)
             transposes(A0, b + 1)
             copies(A0, b + 1)
             message_add(b, 1, 1)
             message_passes(b + 1, 0, 0)
             quantise_messages(b, 0)
-            for s in range(3):
-                self_pass(b, s)
+            for s in range(3 if b < B - 1 else 4):
                 aggregate_pass(b, s, 0)
-            row_sum(b, 3)
             message_add(b, 1, 2)
+            reciprocal_den(b - 1)
+            scale_and_store(b - 1, 0)
+            scale_and_store(b - 1, 1)
+            if b < B - 1:
+                row_sum(b, 1)
             message_add(b, 1, 3)
             quantise(A1, b)
             quantise_messages(b, 1)
-            for s in range(3):
+            for s in range(3 if b < B - 1 else 4):
                 aggregate_pass(b, s, 1)
-            transposes(X, b + 2)
-            copies(X, b + 2)
+            message_passes(b + 1, 0, 1)
+            message_passes(b + 1, 0, 2)
             message_add(b + 1, 0, 0)
             quantise(A0, b + 1)
             finish(b)

@@ -175,7 +175,7 @@ def tile_rgcn_layer_pa_t_kernel(tc, x, adj, wr, br, w0, b0, out):
 
 
         def first_tensor_slot(b):
-            return 0 if b == 0 else S - 1
+            return 0 if b == 0 else S - 2 if b == B - 1 else S - 1
 
         def den_tile(b):
             if ("dsum", b) not in live:
@@ -183,8 +183,9 @@ def tile_rgcn_layer_pa_t_kernel(tc, x, adj, wr, br, w0, b0, out):
             return live[("dsum", b)]
 
         def row_sum(b, s):
-            if s >= first_tensor_slot(b):
+            if s >= first_tensor_slot(b) or ("sum", b, s) in live:
                 return
+            live[("sum", b, s)] = True
             junk = pool["b2"].tile([P, R, N], BF16, name="junk")
             nc.scalar.activation(
                 out=junk[:],
@@ -305,7 +306,7 @@ def tile_rgcn_layer_pa_t_kernel(tc, x, adj, wr, br, w0, b0, out):
                 live[("o", b, s // 2)] = pool["b6"].tile([P, 2, D], F32, name="o_sb")
             o_ap = live[("o", b, s // 2)][:, s % 2, :]
             rd = live[("rden", b)][:, s : s + 1]
-            if b == B - 1 and s == S - 1:
+            if b >= B - 2 and s == S - 1:
                 nc.vector.tensor_scalar(
                     out=o_ap, in0=live[("t", b, s)][:], scalar1=rd, scalar2=0.0, op0=ALU.mult, op1=ALU.max
                 )
@@ -316,40 +317,35 @@ def tile_rgcn_layer_pa_t_kernel(tc, x, adj, wr, br, w0, b0, out):
             load_adj(b + 3)
             load_x(b + 4)
             output_add(b, 0)
-            if b < B - 1:
-                self_pass(b, 3)
-                aggregate_pass(b, 3, 0)
-                aggregate_pass(b, 3, 1)
             transposes(X, b + 2)
             copies(X, b + 2)
-            if b < B - 1:
-                row_sum(b, 2)
+            self_pass(b, 3)
+            aggregate_pass(b, 3, 0)
+            aggregate_pass(b, 3, 1)
+            row_sum(b, 1)
+            row_sum(b, 2)
             if b == B - 2:
                 row_sum(b + 1, 0)
-                row_sum(b + 1, 1)
-            if b == B - 1:
-                reciprocal_den(b)
-                output_scale_relu(b, 0)
             output_add(b, 1)
-            if b == B - 1:
-                output_scale_relu(b, 1)
-                store_pair(b, 0)
             output_add(b, 2)
-            if b == B - 1:
-                output_scale_relu(b, 2)
-                store_slot(b, 2)
             message_add(b + 1, 0, 1)
-            output_add(b, 3)
             message_add(b + 1, 0, 2)
+            output_add(b, 3)
             quantise(X, b + 2)
-            if b == B - 1:
-                output_scale_relu(b, 3)
-                store_slot(b, 3)
 
-        def scale_and_store(b, u):
-            output_scale_relu(b, 2 * u)
-            output_scale_relu(b, 2 * u + 1)
-            store_pair(b, u)
+        def finish_last(b):
+            output_add(b, 0)
+            reciprocal_den(b)
+            output_scale_relu(b, 0)
+            output_add(b, 1)
+            output_scale_relu(b, 1)
+            store_pair(b, 0)
+            output_add(b, 2)
+            output_scale_relu(b, 2)
+            store_slot(b, 2)
+            output_add(b, 3)
+            output_scale_relu(b, 3)
+            store_slot(b, 3)
 
         load_first_x()
         load_weight(0)
@@ -389,20 +385,22 @@ def tile_rgcn_layer_pa_t_kernel(tc, x, adj, wr, br, w0, b0, out):
         transposes(A1, 0)
         message_add(0, 0, 3)
         message_passes(0, 1, 2)
-        regroup_weight(W0, "scalar", 0, D)
+        regroup_weight(W0, "vector", 0, D)
         copies(A1, 0)
         message_add(0, 1, 0)
         message_passes(0, 1, 3)
         message_add(0, 1, 1)
         transposes(X, 1)
         copies(X, 1)
-        quantise(A0, 0)
-        message_add(0, 1, 2)
         quantise_weight(W0, 0, D)
         for s in range(3):
             self_pass(0, s)
+        message_add(0, 1, 2)
+        quantise(A0, 0)
         message_add(0, 1, 3)
         quantise_messages(0, 0)
+        transposes(A0, 1)
+        copies(A0, 1)
         for s in range(3):
             aggregate_pass(0, s, 0)
         quantise(A1, 0)
@@ -413,69 +411,75 @@ def tile_rgcn_layer_pa_t_kernel(tc, x, adj, wr, br, w0, b0, out):
         message_passes(1, 0, 0)
         load_adj(3)
         load_x(4)
+        quantise(A0, 1)
         output_add(0, 0)
+        message_passes(1, 0, 1)
+        message_passes(1, 0, 2)
+        transposes(X, 2)
+        copies(X, 2)
         self_pass(0, 3)
         aggregate_pass(0, 3, 0)
         aggregate_pass(0, 3, 1)
-        transposes(A0, 1)
-        copies(A0, 1)
         output_add(0, 1)
-        message_passes(1, 0, 1)
         message_add(1, 0, 0)
-        message_passes(1, 0, 2)
         output_add(0, 2)
-        transposes(X, 2)
-        copies(X, 2)
-        output_add(0, 3)
         message_add(1, 0, 1)
         message_add(1, 0, 2)
+        output_add(0, 3)
+        quantise(X, 2)
 
         for b in range(1, B):
+            last = b == B - 1
+            slots = S if last else S - 1
             message_passes(b, 0, 3)
+            den_passes(b - 1, 0)
             message_passes(b, 1, 0)
+            den_passes(b - 1, 1)
             message_passes(b, 1, 1)
-            if b == 1:
-                quantise(A0, 1)
             transposes(A1, b)
             copies(A1, b)
             message_add(b, 0, 3)
             message_passes(b, 1, 2)
-            for s in range(S):
-                den_passes(b - 1, s)
+            den_passes(b - 1, 2)
+            den_passes(b - 1, 3)
             den_copy(b - 1)
-            if b < B - 1:
-                row_sum(b, 0)
-            else:
-                row_sum(b, 2)
+            row_sum(b, 1 if last else 0)
             message_add(b, 1, 0)
-            if b == 1:
-                quantise(X, 2)
             message_passes(b, 1, 3)
-            for s in range(3 if b < B - 1 else 4):
+            for s in range(slots):
                 self_pass(b, s)
-            if b == B - 1:
-                den_passes(b, 3)
-                den_copy(b)
             transposes(A0, b + 1)
             copies(A0, b + 1)
             message_add(b, 1, 1)
             message_passes(b + 1, 0, 0)
             quantise_messages(b, 0)
-            for s in range(3 if b < B - 1 else 4):
+            for s in range(slots):
                 aggregate_pass(b, s, 0)
+            if last:
+                den_passes(b, 2)
+                den_passes(b, 3)
             message_add(b, 1, 2)
             reciprocal_den(b - 1)
-            scale_and_store(b - 1, 0)
-            scale_and_store(b - 1, 1)
-            if b < B - 1:
-                row_sum(b, 1)
+            output_scale_relu(b - 1, 0)
+            output_scale_relu(b - 1, 1)
+            store_pair(b - 1, 0)
+            output_scale_relu(b - 1, 2)
+            if not last:
+                output_scale_relu(b - 1, 3)
+                store_pair(b - 1, 1)
             message_add(b, 1, 3)
             quantise(A1, b)
             quantise_messages(b, 1)
-            for s in range(3 if b < B - 1 else 4):
+            for s in range(slots):
                 aggregate_pass(b, s, 1)
-            message_passes(b + 1, 0, 1)
-            message_passes(b + 1, 0, 2)
-            message_add(b + 1, 0, 0)
-            quantise(A0, b + 1)
-            finish(b)
+            if last:
+                den_copy(b)
+                output_scale_relu(b - 1, 3)
+                store_pair(b - 1, 1)
+                finish_last(b)
+            else:
+                message_passes(b + 1, 0, 1)
+                message_passes(b + 1, 0, 2)
+                message_add(b + 1, 0, 0)
+                quantise(A0, b + 1)
+                finish(b)

@@ -323,7 +323,6 @@ def tile_rgcn_layer_pa_t_kernel(tc, x, adj, wr, br, w0, b0, out):
             aggregate_pass(b, 3, 0)
             aggregate_pass(b, 3, 1)
             row_sum(b, 1)
-            row_sum(b, 2)
             if b == B - 2:
                 row_sum(b + 1, 0)
             output_add(b, 1)
@@ -432,18 +431,20 @@ def tile_rgcn_layer_pa_t_kernel(tc, x, adj, wr, br, w0, b0, out):
             last = b == B - 1
             slots = S if last else S - 1
             message_passes(b, 0, 3)
-            den_passes(b - 1, 0)
             message_passes(b, 1, 0)
-            den_passes(b - 1, 1)
             message_passes(b, 1, 1)
             transposes(A1, b)
+            for s in range(S):
+                den_passes(b - 1, s)
             copies(A1, b)
             message_add(b, 0, 3)
             message_passes(b, 1, 2)
-            den_passes(b - 1, 2)
-            den_passes(b - 1, 3)
             den_copy(b - 1)
-            row_sum(b, 1 if last else 0)
+            if last:
+                row_sum(b, 1)
+            else:
+                row_sum(b, 0)
+                row_sum(b, 2)
             message_add(b, 1, 0)
             message_passes(b, 1, 3)
             for s in range(slots):

@@ -301,12 +301,23 @@ def tile_rgcn_layer_pa_t_kernel(tc, x, adj, wr, br, w0, b0, out):
             )
             live[("t", b, s)] = t
 
+        def output_add_beside(b, s):
+            u = pool["b2"].tile([P, D], F32, name="u")
+            nc.scalar.copy(out=u[:], in_=live[("bo", b, s)][:])
+            t = pool["b2"].tile([P, D], F32, name="t_beside")
+            nc.gpsimd.tensor_tensor(out=t[:], in0=u[:], in1=bias[:, W0 * D : (W0 + 1) * D], op=ALU.add)
+            live[("t", b, s)] = t
+
         def output_scale_relu(b, s):
             if ("o", b, s // 2) not in live:
                 live[("o", b, s // 2)] = pool["b6"].tile([P, 2, D], F32, name="o_sb")
             o_ap = live[("o", b, s // 2)][:, s % 2, :]
             rd = live[("rden", b)][:, s : s + 1]
-            if b >= B - 2 and s == S - 1:
+            if 0 < b < B - 2 and s == S - 1:
+                nc.gpsimd.tensor_scalar(
+                    out=o_ap, in0=live[("t", b, s)][:], scalar1=rd, scalar2=0.0, op0=ALU.mult, op1=ALU.max
+                )
+            elif b >= B - 2 and s == S - 1:
                 nc.vector.tensor_scalar(
                     out=o_ap, in0=live[("t", b, s)][:], scalar1=rd, scalar2=0.0, op0=ALU.mult, op1=ALU.max
                 )
@@ -326,11 +337,9 @@ def tile_rgcn_layer_pa_t_kernel(tc, x, adj, wr, br, w0, b0, out):
             if b == B - 2:
                 row_sum(b + 1, 0)
             output_add(b, 1)
-            output_add(b, 2)
             message_add(b + 1, 0, 1)
             message_add(b + 1, 0, 2)
             output_add(b, 3)
-            quantise(X, b + 2)
 
         def finish_last(b):
             output_add(b, 0)
@@ -369,7 +378,8 @@ def tile_rgcn_layer_pa_t_kernel(tc, x, adj, wr, br, w0, b0, out):
         message_passes(0, 0, 1)
         quantise_weight(0, D // 2, D)
         message_passes(0, 0, 2)
-        regroup_weight(1, "scalar", 0, D)
+        regroup_weight(1, "vector", 0, D // 2)
+        regroup_weight(1, "scalar", D // 2, D)
         spread_bias(1)
         spread_bias(W0)
         transposes(A0, 0)
@@ -384,7 +394,8 @@ def tile_rgcn_layer_pa_t_kernel(tc, x, adj, wr, br, w0, b0, out):
         transposes(A1, 0)
         message_add(0, 0, 3)
         message_passes(0, 1, 2)
-        regroup_weight(W0, "vector", 0, D)
+        regroup_weight(W0, "vector", 0, D // 2)
+        regroup_weight(W0, "scalar", D // 2, D)
         copies(A1, 0)
         message_add(0, 1, 0)
         message_passes(0, 1, 3)
@@ -446,6 +457,8 @@ def tile_rgcn_layer_pa_t_kernel(tc, x, adj, wr, br, w0, b0, out):
                 row_sum(b, 0)
                 row_sum(b, 2)
             message_add(b, 1, 0)
+            if b > 1:
+                quantise(X, b + 1)
             message_passes(b, 1, 3)
             for s in range(slots):
                 self_pass(b, s)
@@ -464,10 +477,8 @@ def tile_rgcn_layer_pa_t_kernel(tc, x, adj, wr, br, w0, b0, out):
             output_scale_relu(b - 1, 0)
             output_scale_relu(b - 1, 1)
             store_pair(b - 1, 0)
-            output_scale_relu(b - 1, 2)
-            if not last:
-                output_scale_relu(b - 1, 3)
-                store_pair(b - 1, 1)
+            if last:
+                output_scale_relu(b - 1, 2)
             message_add(b, 1, 3)
             quantise(A1, b)
             quantise_messages(b, 1)
@@ -481,6 +492,10 @@ def tile_rgcn_layer_pa_t_kernel(tc, x, adj, wr, br, w0, b0, out):
             else:
                 message_passes(b + 1, 0, 1)
                 message_passes(b + 1, 0, 2)
+                output_add_beside(b, 2)
+                output_scale_relu(b - 1, 2)
+                output_scale_relu(b - 1, 3)
+                store_pair(b - 1, 1)
                 message_add(b + 1, 0, 0)
                 quantise(A0, b + 1)
                 finish(b)

@@ -301,23 +301,12 @@ def tile_rgcn_layer_pa_t_kernel(tc, x, adj, wr, br, w0, b0, out):
             )
             live[("t", b, s)] = t
 
-        def output_add_beside(b, s):
-            u = pool["b2"].tile([P, D], F32, name="u")
-            nc.scalar.copy(out=u[:], in_=live[("bo", b, s)][:])
-            t = pool["b2"].tile([P, D], F32, name="t_beside")
-            nc.gpsimd.tensor_tensor(out=t[:], in0=u[:], in1=bias[:, W0 * D : (W0 + 1) * D], op=ALU.add)
-            live[("t", b, s)] = t
-
         def output_scale_relu(b, s):
             if ("o", b, s // 2) not in live:
                 live[("o", b, s // 2)] = pool["b6"].tile([P, 2, D], F32, name="o_sb")
             o_ap = live[("o", b, s // 2)][:, s % 2, :]
             rd = live[("rden", b)][:, s : s + 1]
-            if 0 < b < B - 2 and s == S - 1:
-                nc.gpsimd.tensor_scalar(
-                    out=o_ap, in0=live[("t", b, s)][:], scalar1=rd, scalar2=0.0, op0=ALU.mult, op1=ALU.max
-                )
-            elif b >= B - 2 and s == S - 1:
+            if b >= B - 2 and s == S - 1:
                 nc.vector.tensor_scalar(
                     out=o_ap, in0=live[("t", b, s)][:], scalar1=rd, scalar2=0.0, op0=ALU.mult, op1=ALU.max
                 )
@@ -334,12 +323,15 @@ def tile_rgcn_layer_pa_t_kernel(tc, x, adj, wr, br, w0, b0, out):
             aggregate_pass(b, 3, 0)
             aggregate_pass(b, 3, 1)
             row_sum(b, 1)
+            row_sum(b, 2)
             if b == B - 2:
                 row_sum(b + 1, 0)
             output_add(b, 1)
+            output_add(b, 2)
             message_add(b + 1, 0, 1)
             message_add(b + 1, 0, 2)
             output_add(b, 3)
+            quantise(X, b + 2)
 
         def finish_last(b):
             output_add(b, 0)
@@ -451,14 +443,8 @@ def tile_rgcn_layer_pa_t_kernel(tc, x, adj, wr, br, w0, b0, out):
             message_add(b, 0, 3)
             message_passes(b, 1, 2)
             den_copy(b - 1)
-            if last:
-                row_sum(b, 1)
-            else:
-                row_sum(b, 0)
-                row_sum(b, 2)
+            row_sum(b, 1 if last else 0)
             message_add(b, 1, 0)
-            if b > 1:
-                quantise(X, b + 1)
             message_passes(b, 1, 3)
             for s in range(slots):
                 self_pass(b, s)
@@ -477,8 +463,10 @@ def tile_rgcn_layer_pa_t_kernel(tc, x, adj, wr, br, w0, b0, out):
             output_scale_relu(b - 1, 0)
             output_scale_relu(b - 1, 1)
             store_pair(b - 1, 0)
-            if last:
-                output_scale_relu(b - 1, 2)
+            output_scale_relu(b - 1, 2)
+            if not last:
+                output_scale_relu(b - 1, 3)
+                store_pair(b - 1, 1)
             message_add(b, 1, 3)
             quantise(A1, b)
             quantise_messages(b, 1)
@@ -492,10 +480,6 @@ def tile_rgcn_layer_pa_t_kernel(tc, x, adj, wr, br, w0, b0, out):
             else:
                 message_passes(b + 1, 0, 1)
                 message_passes(b + 1, 0, 2)
-                output_add_beside(b, 2)
-                output_scale_relu(b - 1, 2)
-                output_scale_relu(b - 1, 3)
-                store_pair(b - 1, 1)
                 message_add(b + 1, 0, 0)
                 quantise(A0, b + 1)
                 finish(b)

@@ -33,7 +33,7 @@ def tile_rgcn_layer_pa_t_kernel(tc, x, adj, wr, br, w0, b0, out):
         make_identity(nc, ident[:])
         ctx.enter_context(tc.manual_schedule())
 
-        ones = const.tile([P, P], BF16, name="ones")
+        ones = const.tile([P, D], BF16, name="ones")
         share = const.tile([P, 1], BF16, name="share")
         zb = const.tile([P, 3 * D], BF16, name="zb")
         bias = const.tile([P, 3 * D], BF16, name="bias")
@@ -82,8 +82,8 @@ def tile_rgcn_layer_pa_t_kernel(tc, x, adj, wr, br, w0, b0, out):
             )
 
         def load_bias_rows():
-            nc.vector.memset(zb[:], 0.0)
             nc.vector.memset(ones[:], 1.0)
+            nc.vector.memset(zb[:], 0.0)
             nc.vector.memset(share[:], 1.0 / P)
             nc.sync.dma_start(out=zb[0:1, 0 : R * D], in_=br.rearrange("r d -> (r d)").unsqueeze(0))
             nc.sync.dma_start(out=zb[0:1, R * D : 3 * D], in_=b0.unsqueeze(0))
@@ -107,9 +107,14 @@ def tile_rgcn_layer_pa_t_kernel(tc, x, adj, wr, br, w0, b0, out):
             else:
                 nc.vector.tensor_copy(out=out_ap, in_=in_ap)
 
+        def keep_busy(passes):
+            bank = ps_o.tile([P, D], F32, name="bank_o")
+            for i in range(passes):
+                nc.tensor.matmul(out=bank[:], lhsT=ones[:, 0:P], rhs=ones[:], start=True, stop=True)
+
         def spread_bias(w):
             bank = ps_o.tile([P, D], F32, name="bank_o")
-            nc.tensor.matmul(out=bank[:], lhsT=ones[:], rhs=zb[:, w * D : (w + 1) * D], start=True, stop=True)
+            nc.tensor.matmul(out=bank[:], lhsT=ones[:, 0:P], rhs=zb[:, w * D : (w + 1) * D], start=True, stop=True)
             nc.scalar.copy(out=bias[:, w * D : (w + 1) * D], in_=bank[:])
 
         def regroup_weight(w, engine, c0, c1):
@@ -215,7 +220,7 @@ def tile_rgcn_layer_pa_t_kernel(tc, x, adj, wr, br, w0, b0, out):
                         start=(r == 0 and t == 0),
                         stop=False,
                     )
-            nc.tensor.matmul(out=bank[:, s : s + 1], lhsT=ones[:], rhs=share[:], start=False, stop=True)
+            nc.tensor.matmul(out=bank[:, s : s + 1], lhsT=ones[:, 0:P], rhs=share[:], start=False, stop=True)
 
         def den_copy(b):
             s0 = first_tensor_slot(b)
@@ -358,12 +363,15 @@ def tile_rgcn_layer_pa_t_kernel(tc, x, adj, wr, br, w0, b0, out):
         load_x(2)
         load_adj(2)
         load_x(3)
+        keep_busy(4)
         transposes(X, 0)
+        keep_busy(3)
         copy_half(X, 0, 0, "scalar")
         copy_half(X, 0, 1, "vector")
         regroup_weight(0, "vector", 0, D // 2)
         regroup_weight(0, "scalar", D // 2, D)
         spread_bias(0)
+        keep_busy(2)
         quantise(X, 0)
         quantise_weight(0, 0, D // 2)
         message_passes(0, 0, 0)

@@ -23,7 +23,7 @@ def tile_rgcn_layer_pa_t_kernel(tc, x, adj, wr, br, w0, b0, out):
     nc = tc.nc
     with ExitStack() as ctx:
         pool = {}
-        for name, bufs in (("const", 1), ("b2", 2), ("b3", 3), ("b4", 4), ("b6", 6)):
+        for name, bufs in (("const", 1), ("b2", 2), ("b3", 3), ("b4", 4), ("b6", 6), ("b8", 8)):
             pool[name] = ctx.enter_context(tc.tile_pool(name=name, bufs=bufs))
         ps_t = ctx.enter_context(tc.psum_pool(name="ps_t", bufs=2))
         ps_m = ctx.enter_context(tc.psum_pool(name="ps_m", bufs=3))
@@ -300,7 +300,7 @@ def tile_rgcn_layer_pa_t_kernel(tc, x, adj, wr, br, w0, b0, out):
             )
 
         def output_add(b, s):
-            t = pool["b6"].tile([P, D], F32, name="t")
+            t = pool["b8"].tile([P, D], F32, name="t")
             nc.vector.tensor_tensor(
                 out=t[:], in0=live[("bo", b, s)][:], in1=bias[:, W0 * D : (W0 + 1) * D], op=ALU.add
             )

@@ -180,7 +180,7 @@ def tile_rgcn_layer_pa_t_kernel(tc, x, adj, wr, br, w0, b0, out):
 
 
         def first_tensor_slot(b):
-            return 0 if b == 0 else S - 2 if b == B - 1 else S - 1
+            return 0 if b == 0 else S - 2
 
         def den_tile(b):
             if ("dsum", b) not in live:
@@ -306,6 +306,13 @@ def tile_rgcn_layer_pa_t_kernel(tc, x, adj, wr, br, w0, b0, out):
             )
             live[("t", b, s)] = t
 
+        def output_add_beside(b, s):
+            u = pool["b2"].tile([P, D], F32, name="u")
+            nc.scalar.copy(out=u[:], in_=live[("bo", b, s)][:])
+            t = pool["b2"].tile([P, D], F32, name="t_beside")
+            nc.gpsimd.tensor_tensor(out=t[:], in0=u[:], in1=bias[:, W0 * D : (W0 + 1) * D], op=ALU.add)
+            live[("t", b, s)] = t
+
         def output_scale_relu(b, s):
             if ("o", b, s // 2) not in live:
                 live[("o", b, s // 2)] = pool["b6"].tile([P, 2, D], F32, name="o_sb")
@@ -321,12 +328,11 @@ def tile_rgcn_layer_pa_t_kernel(tc, x, adj, wr, br, w0, b0, out):
         def finish(b):
             load_adj(b + 3)
             load_x(b + 4)
-            output_add(b, 0)
-            transposes(X, b + 2)
-            copies(X, b + 2)
             self_pass(b, 3)
             aggregate_pass(b, 3, 0)
             aggregate_pass(b, 3, 1)
+            transposes(X, b + 2)
+            copies(X, b + 2)
             row_sum(b, 1)
             row_sum(b, 2)
             if b == B - 2:
@@ -336,7 +342,6 @@ def tile_rgcn_layer_pa_t_kernel(tc, x, adj, wr, br, w0, b0, out):
             message_add(b + 1, 0, 1)
             message_add(b + 1, 0, 2)
             output_add(b, 3)
-            quantise(X, b + 2)
 
         def finish_last(b):
             output_add(b, 0)
@@ -453,6 +458,8 @@ def tile_rgcn_layer_pa_t_kernel(tc, x, adj, wr, br, w0, b0, out):
             den_copy(b - 1)
             row_sum(b, 1 if last else 0)
             message_add(b, 1, 0)
+            if b > 1:
+                quantise(X, b + 1)
             message_passes(b, 1, 3)
             for s in range(slots):
                 self_pass(b, s)
@@ -468,13 +475,12 @@ def tile_rgcn_layer_pa_t_kernel(tc, x, adj, wr, br, w0, b0, out):
                 den_passes(b, 3)
             message_add(b, 1, 2)
             reciprocal_den(b - 1)
-            output_scale_relu(b - 1, 0)
-            output_scale_relu(b - 1, 1)
-            store_pair(b - 1, 0)
-            output_scale_relu(b - 1, 2)
-            if not last:
-                output_scale_relu(b - 1, 3)
-                store_pair(b - 1, 1)
+            for s in range(1):
+                output_scale_relu(b - 1, s)
+            if last:
+                for s in range(1, 3):
+                    output_scale_relu(b - 1, s)
+                store_pair(b - 1, 0)
             message_add(b, 1, 3)
             quantise(A1, b)
             quantise_messages(b, 1)
@@ -488,6 +494,11 @@ def tile_rgcn_layer_pa_t_kernel(tc, x, adj, wr, br, w0, b0, out):
             else:
                 message_passes(b + 1, 0, 1)
                 message_passes(b + 1, 0, 2)
+                output_add_beside(b, 0)
+                for s in range(1, S):
+                    output_scale_relu(b - 1, s)
+                store_pair(b - 1, 0)
+                store_pair(b - 1, 1)
                 message_add(b + 1, 0, 0)
                 quantise(A0, b + 1)
                 finish(b)

@@ -34,7 +34,6 @@ def tile_rgcn_layer_pa_t_kernel(tc, x, adj, wr, br, w0, b0, out):
         ctx.enter_context(tc.manual_schedule())
 
         ones = const.tile([P, D], BF16, name="ones")
-        share = const.tile([P, 1], BF16, name="share")
         zb = const.tile([P, 3 * D], BF16, name="zb")
         bias = const.tile([P, 3 * D], BF16, name="bias")
         w_raw = const.tile([P, 3, S, D], BF16, name="w_raw")
@@ -84,7 +83,6 @@ def tile_rgcn_layer_pa_t_kernel(tc, x, adj, wr, br, w0, b0, out):
         def load_bias_rows():
             nc.vector.memset(ones[:], 1.0)
             nc.vector.memset(zb[:], 0.0)
-            nc.vector.memset(share[:], 1.0 / P)
             nc.sync.dma_start(out=zb[0:1, 0 : R * D], in_=br.rearrange("r d -> (r d)").unsqueeze(0))
             nc.sync.dma_start(out=zb[0:1, R * D : 3 * D], in_=b0.unsqueeze(0))
 
@@ -113,7 +111,7 @@ def tile_rgcn_layer_pa_t_kernel(tc, x, adj, wr, br, w0, b0, out):
                 nc.tensor.matmul(out=bank[:], lhsT=ones[:, 0:P], rhs=ones[:], start=True, stop=True)
 
         def spread_bias(w):
-            bank = ps_o.tile([P, D], F32, name="bank_o")
+            bank = ps_o.tile([P, D], BF16, name="bank_o")
             nc.tensor.matmul(out=bank[:], lhsT=ones[:, 0:P], rhs=zb[:, w * D : (w + 1) * D], start=True, stop=True)
             nc.scalar.copy(out=bias[:, w * D : (w + 1) * D], in_=bank[:])
 
@@ -218,13 +216,12 @@ def tile_rgcn_layer_pa_t_kernel(tc, x, adj, wr, br, w0, b0, out):
                         lhsT=nodes[:, s * P : (s + 1) * P, t],
                         rhs=ones[:, 0:1],
                         start=(r == 0 and t == 0),
-                        stop=False,
+                        stop=(r == R - 1 and t == S - 1),
                     )
-            nc.tensor.matmul(out=bank[:, s : s + 1], lhsT=ones[:, 0:P], rhs=share[:], start=False, stop=True)
 
         def den_copy(b):
             s0 = first_tensor_slot(b)
-            nc.scalar.copy(out=den_tile(b)[:, s0:S], in_=live[("den", b)][:, s0:S])
+            nc.scalar.activation(out=den_tile(b)[:, s0:S], in_=live[("den", b)][:, s0:S], func=ACT.Copy, bias=1.0)
 
         def reciprocal_den(b):
             rden = pool["b3"].tile([P, S], F32, name="rden")
@@ -427,7 +424,7 @@ def tile_rgcn_layer_pa_t_kernel(tc, x, adj, wr, br, w0, b0, out):
         load_adj(3)
         load_x(4)
         quantise(A0, 1)
-        output_add(0, 0)
+        output_add_beside(0, 0)
         message_passes(1, 0, 1)
         message_passes(1, 0, 2)
         transposes(X, 2)
@@ -458,16 +455,16 @@ def tile_rgcn_layer_pa_t_kernel(tc, x, adj, wr, br, w0, b0, out):
             den_copy(b - 1)
             row_sum(b, 1 if last else 0)
             message_add(b, 1, 0)
-            if b > 1:
-                quantise(X, b + 1)
             message_passes(b, 1, 3)
             for s in range(slots):
                 self_pass(b, s)
             transposes(A0, b + 1)
             copies(A0, b + 1)
             message_add(b, 1, 1)
-            message_passes(b + 1, 0, 0)
+            if b > 1:
+                quantise(X, b + 1)
             quantise_messages(b, 0)
+            message_passes(b + 1, 0, 0)
             for s in range(slots):
                 aggregate_pass(b, s, 0)
             if last:

from contextlib import ExitStack

import concourse.mybir as mybir
from concourse.masks import make_identity

F32 = mybir.dt.float32
BF16 = mybir.dt.bfloat16
U32 = mybir.dt.uint32
U8 = mybir.dt.uint8
FP8X4 = mybir.dt.float8_e4m3fn_x4
ALU = mybir.AluOpType
ACT = mybir.ActivationFunctionType

B, R, N, D = 8, 2, 512, 512
P = 128
S = 4
X, A0, A1 = 0, 1, 2
W0 = R
FLOPS = 2 * B * (R * N * D * D + N * R * N * D + N * D * D)


def tile_rgcn_layer_pa_t_kernel(tc, x, adj, wr, br, w0, b0, out):
    nc = tc.nc
    with ExitStack() as ctx:
        pool = {}
        for name, bufs in (("const", 1), ("b2", 2), ("b3", 3), ("b4", 4), ("b6", 6), ("b8", 8)):
            pool[name] = ctx.enter_context(tc.tile_pool(name=name, bufs=bufs))
        ps_t = ctx.enter_context(tc.psum_pool(name="ps_t", bufs=2))
        ps_m = ctx.enter_context(tc.psum_pool(name="ps_m", bufs=3))
        ps_o = ctx.enter_context(tc.psum_pool(name="ps_o", bufs=3))
        const = pool["const"]
        ident = const.tile([P, P], F32, name="ident")
        make_identity(nc, ident[:])
        ctx.enter_context(tc.manual_schedule())

        ones = const.tile([P, D], BF16, name="ones")
        zb = const.tile([P, 3 * D], BF16, name="zb")
        bias = const.tile([P, 3 * D], BF16, name="bias")
        w_raw = const.tile([P, 3, S, D], BF16, name="w_raw")
        w_grp = const.tile([P, 3, D, S], BF16, name="w_grp", align_bytes=64)
        w_words = const.tile([P, 3 * D], U32, name="w_words", align_bytes=64)
        w_scales = const.tile([P, 3 * D], U8, name="w_scales", align_bytes=64)

        live = {}


        def load_x(k):
            if k >= B:
                return
            x_sb = pool["b4"].tile([P, S, D], BF16, name="x_sb")
            nc.sync.dma_start(
                out=x_sb[:].rearrange("p (u e) f -> p u (e f)", u=2),
                in_=x[k].rearrange("(u p e) f -> p u (e f)", u=2, e=2),
            )
            live[("x", k)] = x_sb

        def load_first_x():
            x_sb = pool["b4"].tile([P, S, D], BF16, name="x_sb")
            for u in range(2):
                nc.sync.dma_start(
                    out=x_sb[:, 2 * u : 2 * u + 2, :].rearrange("p e f -> p (e f)"),
                    in_=x[0, 256 * u : 256 * (u + 1), :].rearrange("(p e) f -> p (e f)", e=2),
                )
            live[("x", 0)] = x_sb

        def load_adj(k):
            if k >= B:
                return
            a_sb = pool["b4"].tile([P, R, S, N], BF16, name="a_sb")
            nc.sync.dma_start(
                out=a_sb[:].rearrange("p r (u e) j -> p (r u) (e j)", u=2),
                in_=adj[k].rearrange("r (u p e) j -> p (r u) (e j)", u=2, e=2),
            )
            live[("a", k)] = a_sb

        def load_weight(w):
            src = wr[w] if w < R else w0
            nc.sync.dma_start(
                out=w_raw[:, w].rearrange("p (u e) c -> p u (e c)", u=2),
                in_=src.rearrange("(u p e) c -> p u (e c)", u=2, e=2),
            )

        def load_bias_rows():
            nc.vector.memset(ones[:], 1.0)
            nc.vector.memset(zb[:], 0.0)
            nc.sync.dma_start(out=zb[0:1, 0 : R * D], in_=br.rearrange("r d -> (r d)").unsqueeze(0))
            nc.sync.dma_start(out=zb[0:1, R * D : 3 * D], in_=b0.unsqueeze(0))

        def store_pair(b, u):
            nc.sync.dma_start(
                out=out[b, 256 * u : 256 * (u + 1), :].rearrange("(p e) d -> p (e d)", e=2),
                in_=live[("o", b, u)][:].rearrange("p e d -> p (e d)"),
            )

        def store_slot(b, s):
            nc.sync.dma_start(
                out=out[b, 256 * (s // 2) : 256 * (s // 2 + 1), :].rearrange("(p e) d -> p e d", e=2)[:, s % 2, :],
                in_=live[("o", b, s // 2)][:, s % 2, :],
            )


        def copy_on(engine, out_ap, in_ap):
            if engine == "scalar":
                nc.scalar.copy(out=out_ap, in_=in_ap)
            else:
                nc.vector.tensor_copy(out=out_ap, in_=in_ap)

        def keep_busy(passes):
            bank = ps_o.tile([P, D], F32, name="bank_o")
            for i in range(passes):
                nc.tensor.matmul(out=bank[:], lhsT=ones[:, 0:P], rhs=ones[:], start=True, stop=True)

        def spread_bias(w):
            bank = ps_o.tile([P, D], BF16, name="bank_o")
            nc.tensor.matmul(out=bank[:], lhsT=ones[:, 0:P], rhs=zb[:, w * D : (w + 1) * D], start=True, stop=True)
            nc.scalar.copy(out=bias[:, w * D : (w + 1) * D], in_=bank[:])

        def regroup_weight(w, engine, c0, c1):
            copy_on(
                engine,
                w_grp[:, w, c0:c1, :].rearrange("p (c i) t -> p c t i", i=4),
                w_raw[:, w, :, c0:c1].rearrange("p t (c i) -> p c t i", i=4),
            )

        def quantise_weight(w, c0, c1):
            nc.vector.quantize_mx(
                out=w_words[:, w * D + c0 : w * D + c1].bitcast(FP8X4),
                scales=w_scales[:, w * D + c0 : w * D + c1],
                in_=w_grp[:, w, c0:c1, :].rearrange("p c t -> p (c t)"),
            )


        def transpose_half(m, k, h):
            if m == X:
                words = live[("x", k)][:].bitcast(F32)
            else:
                words = live[("a", k)][:].bitcast(F32)[:, m - 1]
            bank = ps_t.tile([P, 2, 256], F32, name="bank_t")
            for sl in range(2):
                for u in range(2):
                    nc.tensor.transpose(
                        bank[:, u, sl * P : (sl + 1) * P], words[:, 2 * h + sl, u * P : (u + 1) * P], ident[:]
                    )
            live[("bt", m, k, h)] = bank

        def transposes(m, k):
            if k < B:
                transpose_half(m, k, 0)
                transpose_half(m, k, 1)

        def copy_half(m, k, h, engine):
            if h == 0:
                live[("g", m, k)] = pool["b2"].tile([P, 512, 2], F32, name="g%d" % m, align_bytes=64)
            copy_on(
                engine,
                live[("g", m, k)][:, h * 256 : (h + 1) * 256, :],
                live[("bt", m, k, h)][:].rearrange("p w c -> p c w"),
            )

        def copies(m, k):
            if k < B:
                copy_half(m, k, 0, "scalar")
                copy_half(m, k, 1, "scalar")

        def quantise_tile(grouped, tag, depth):
            words = pool[depth].tile([P, 512], U32, name="w_" + tag, align_bytes=64)
            scales = pool[depth].tile([P, 512], U8, name="s_" + tag, align_bytes=64)
            nc.vector.quantize_mx(out=words[:].bitcast(FP8X4), scales=scales[:], in_=grouped)
            return words, scales

        def quantise(m, k):
            if k < B:
                live[("q", m, k)] = quantise_tile(
                    live[("g", m, k)][:].rearrange("p c w -> p (c w)").bitcast(BF16),
                    "q%d" % m,
                    "b3" if m == X else "b2",
                )


        def first_tensor_slot(b):
            return 0 if b == 0 else S - 2

        def den_tile(b):
            if ("dsum", b) not in live:
                live[("dsum", b)] = pool["b3"].tile([P, S], F32, name="dsum")
            return live[("dsum", b)]

        def row_sum(b, s):
            if s >= first_tensor_slot(b) or ("sum", b, s) in live:
                return
            live[("sum", b, s)] = True
            junk = pool["b2"].tile([P, R, N], BF16, name="junk")
            nc.scalar.activation(
                out=junk[:],
                in_=live[("a", b)][:, :, s, :],
                func=ACT.Copy,
                bias=1.0 / (R * N),
                accum_out=den_tile(b)[:, s : s + 1],
            )

        def den_passes(b, s):
            if s < first_tensor_slot(b):
                return
            if ("den", b) not in live:
                if b < B - 1:
                    live[("den", b)] = ps_o.tile([P, S], F32, name="bank_o")
                else:
                    live[("den", b)] = ps_t.tile([P, S], F32, name="bank_t")
            bank = live[("den", b)]
            for r in range(R):
                nodes = live[("g", A0 + r, b)][:].rearrange("p c w -> p (c w)").bitcast(BF16)
                nodes = nodes.rearrange("p (c t) -> p c t", t=S)
                for t in range(S):
                    nc.tensor.matmul(
                        out=bank[:, s : s + 1],
                        lhsT=nodes[:, s * P : (s + 1) * P, t],
                        rhs=ones[:, 0:1],
                        start=(r == 0 and t == 0),
                        stop=(r == R - 1 and t == S - 1),
                    )

        def den_copy(b):
            s0 = first_tensor_slot(b)
            nc.scalar.activation(out=den_tile(b)[:, s0:S], in_=live[("den", b)][:, s0:S], func=ACT.Copy, bias=1.0)

        def reciprocal_den(b):
            rden = pool["b3"].tile([P, S], F32, name="rden")
            nc.vector.reciprocal(rden[:], live[("dsum", b)][:])
            live[("rden", b)] = rden


        def message_passes(b, r, dc):
            if b >= B:
                return
            xw, xs = live[("q", X, b)]
            bank = ps_m.tile([P, S, P], F32, name="bank_m")
            cols = slice(r * D + dc * P, r * D + (dc + 1) * P)
            for s in range(S):
                nc.tensor.matmul_mx(
                    out=bank[:, s, :],
                    lhsT=xw[:, s * P : (s + 1) * P].bitcast(FP8X4),
                    lhsT_scale=xs[:, s * P : (s + 1) * P],
                    rhs=w_words[:, cols].bitcast(FP8X4),
                    rhs_scale=w_scales[:, cols],
                    start=True,
                    stop=True,
                )
            live[("bm", b, r, dc)] = bank

        def message_add(b, r, dc):
            if b >= B:
                return
            if dc == 0:
                live[("mg", b, r)] = pool["b2"].tile([P, D, S], BF16, name="mg", align_bytes=64)
            cols = slice(r * D + dc * P, r * D + (dc + 1) * P)
            nc.vector.tensor_tensor(
                out=live[("mg", b, r)][:, dc * P : (dc + 1) * P, :],
                in0=live[("bm", b, r, dc)][:].rearrange("p s d -> p d s"),
                in1=bias[:, cols].unsqueeze(2).to_broadcast([P, P, S]),
                op=ALU.add,
            )

        def quantise_messages(b, r):
            live[("qm", b, r)] = quantise_tile(live[("mg", b, r)][:].rearrange("p d s -> p (d s)"), "qm%d" % r, "b2")


        def self_pass(b, s):
            xw, xs = live[("q", X, b)]
            rows = slice(s * P, (s + 1) * P)
            if s < S - 1 or b < B - 1:
                bank = ps_o.tile([P, D], F32, name="bank_o")
            else:
                bank = ps_t.tile([P, D], F32, name="bank_t")
            nc.tensor.matmul_mx(
                out=bank[:],
                lhsT=xw[:, rows].bitcast(FP8X4),
                lhsT_scale=xs[:, rows],
                rhs=w_words[:, W0 * D : (W0 + 1) * D].bitcast(FP8X4),
                rhs_scale=w_scales[:, W0 * D : (W0 + 1) * D],
                start=True,
                stop=False,
            )
            live[("bo", b, s)] = bank

        def aggregate_pass(b, s, r):
            rows = slice(s * P, (s + 1) * P)
            aw, asc = live[("q", A0 + r, b)]
            mw, msc = live[("qm", b, r)]
            nc.tensor.matmul_mx(
                out=live[("bo", b, s)][:],
                lhsT=aw[:, rows].bitcast(FP8X4),
                lhsT_scale=asc[:, rows],
                rhs=mw[:].bitcast(FP8X4),
                rhs_scale=msc[:],
                start=False,
                stop=(r == R - 1),
            )

        def output_add(b, s):
            t = pool["b8"].tile([P, D], F32, name="t")
            nc.vector.tensor_tensor(
                out=t[:], in0=live[("bo", b, s)][:], in1=bias[:, W0 * D : (W0 + 1) * D], op=ALU.add
            )
            live[("t", b, s)] = t

        def output_add_beside(b, s):
            u = pool["b2"].tile([P, D], F32, name="u")
            nc.scalar.copy(out=u[:], in_=live[("bo", b, s)][:])
            t = pool["b2"].tile([P, D], F32, name="t_beside")
            nc.gpsimd.tensor_tensor(out=t[:], in0=u[:], in1=bias[:, W0 * D : (W0 + 1) * D], op=ALU.add)
            live[("t", b, s)] = t

        def output_scale_relu(b, s):
            if ("o", b, s // 2) not in live:
                live[("o", b, s // 2)] = pool["b6"].tile([P, 2, D], F32, name="o_sb")
            o_ap = live[("o", b, s // 2)][:, s % 2, :]
            rd = live[("rden", b)][:, s : s + 1]
            if b >= B - 2 and s == S - 1:
                nc.vector.tensor_scalar(
                    out=o_ap, in0=live[("t", b, s)][:], scalar1=rd, scalar2=0.0, op0=ALU.mult, op1=ALU.max
                )
            else:
                nc.scalar.activation(out=o_ap, in_=live[("t", b, s)][:], func=ACT.Relu, scale=rd)

        def finish(b):
            load_adj(b + 3)
            load_x(b + 4)
            self_pass(b, 3)
            aggregate_pass(b, 3, 0)
            aggregate_pass(b, 3, 1)
            transposes(X, b + 2)
            copies(X, b + 2)
            row_sum(b, 1)
            row_sum(b, 2)
            if b == B - 2:
                row_sum(b + 1, 0)
            output_add(b, 1)
            output_add(b, 2)
            message_add(b + 1, 0, 1)
            message_add(b + 1, 0, 2)
            output_add(b, 3)

        def finish_last(b):
            output_add(b, 0)
            reciprocal_den(b)
            output_scale_relu(b, 0)
            output_add(b, 1)
            output_scale_relu(b, 1)
            store_pair(b, 0)
            output_add(b, 2)
            output_scale_relu(b, 2)
            store_slot(b, 2)
            output_add(b, 3)
            output_scale_relu(b, 3)
            store_slot(b, 3)

        load_first_x()
        load_weight(0)
        load_bias_rows()
        load_weight(1)
        load_adj(0)
        load_weight(W0)
        load_x(1)
        load_adj(1)
        load_x(2)
        load_adj(2)
        load_x(3)
        keep_busy(4)
        transposes(X, 0)
        keep_busy(3)
        copy_half(X, 0, 0, "scalar")
        copy_half(X, 0, 1, "vector")
        regroup_weight(0, "vector", 0, D // 2)
        regroup_weight(0, "scalar", D // 2, D)
        spread_bias(0)
        keep_busy(2)
        quantise(X, 0)
        quantise_weight(0, 0, D // 2)
        message_passes(0, 0, 0)
        message_passes(0, 0, 1)
        quantise_weight(0, D // 2, D)
        message_passes(0, 0, 2)
        regroup_weight(1, "vector", 0, D // 2)
        regroup_weight(1, "scalar", D // 2, D)
        spread_bias(1)
        spread_bias(W0)
        transposes(A0, 0)
        message_add(0, 0, 0)
        message_passes(0, 0, 3)
        message_add(0, 0, 1)
        message_add(0, 0, 2)
        quantise_weight(1, 0, D)
        message_passes(0, 1, 0)
        message_passes(0, 1, 1)
        copies(A0, 0)
        transposes(A1, 0)
        message_add(0, 0, 3)
        message_passes(0, 1, 2)
        regroup_weight(W0, "vector", 0, D // 2)
        regroup_weight(W0, "scalar", D // 2, D)
        copies(A1, 0)
        message_add(0, 1, 0)
        message_passes(0, 1, 3)
        message_add(0, 1, 1)
        transposes(X, 1)
        copies(X, 1)
        quantise_weight(W0, 0, D)
        for s in range(3):
            self_pass(0, s)
        message_add(0, 1, 2)
        quantise(A0, 0)
        message_add(0, 1, 3)
        quantise_messages(0, 0)
        transposes(A0, 1)
        copies(A0, 1)
        for s in range(3):
            aggregate_pass(0, s, 0)
        quantise(A1, 0)
        quantise_messages(0, 1)
        for s in range(3):
            aggregate_pass(0, s, 1)
        quantise(X, 1)
        message_passes(1, 0, 0)
        load_adj(3)
        load_x(4)
        quantise(A0, 1)
        output_add_beside(0, 0)
        message_passes(1, 0, 1)
        message_passes(1, 0, 2)
        transposes(X, 2)
        copies(X, 2)
        self_pass(0, 3)
        aggregate_pass(0, 3, 0)
        aggregate_pass(0, 3, 1)
        output_add(0, 1)
        message_add(1, 0, 0)
        output_add(0, 2)
        message_add(1, 0, 1)
        message_add(1, 0, 2)
        output_add(0, 3)
        quantise(X, 2)

        for b in range(1, B):
            last = b == B - 1
            slots = S if last else S - 1
            message_passes(b, 0, 3)
            message_passes(b, 1, 0)
            message_passes(b, 1, 1)
            transposes(A1, b)
            for s in range(S):
                den_passes(b - 1, s)
            copies(A1, b)
            message_add(b, 0, 3)
            message_passes(b, 1, 2)
            den_copy(b - 1)
            row_sum(b, 1 if last else 0)
            message_add(b, 1, 0)
            message_passes(b, 1, 3)
            for s in range(slots):
                self_pass(b, s)
            transposes(A0, b + 1)
            copies(A0, b + 1)
            message_add(b, 1, 1)
            if b > 1:
                quantise(X, b + 1)
            quantise_messages(b, 0)
            message_passes(b + 1, 0, 0)
            for s in range(slots):
                aggregate_pass(b, s, 0)
            if last:
                den_passes(b, 2)
                den_passes(b, 3)
            message_add(b, 1, 2)
            reciprocal_den(b - 1)
            for s in range(1):
                output_scale_relu(b - 1, s)
            if last:
                for s in range(1, 3):
                    output_scale_relu(b - 1, s)
                store_pair(b - 1, 0)
            message_add(b, 1, 3)
            quantise(A1, b)
            quantise_messages(b, 1)
            for s in range(slots):
                aggregate_pass(b, s, 1)
            if last:
                den_copy(b)
                output_scale_relu(b - 1, 3)
                store_pair(b - 1, 1)
                finish_last(b)
            else:
                message_passes(b + 1, 0, 1)
                message_passes(b + 1, 0, 2)
                output_add_beside(b, 0)
                for s in range(1, S):
                    output_scale_relu(b - 1, s)
                store_pair(b - 1, 0)
                store_pair(b - 1, 1)
                message_add(b + 1, 0, 0)
                quantise(A0, b + 1)
                finish(b)
